import numpy as np
import ml_dtypes


def mxq(x, axis, fmt="e4m3"):
    dtype, down = {"e4m3": (ml_dtypes.float8_e4m3fn, 7), "e5m2": (ml_dtypes.float8_e5m2, 14)}[fmt]
    v = np.moveaxis(np.asarray(x, np.float32).astype(ml_dtypes.bfloat16).astype(np.float64), axis, -1)
    blocks = v.reshape(v.shape[:-1] + (-1, 32))
    amax = np.abs(blocks).max(-1, keepdims=True)
    byte = np.maximum(np.where(amax > 0, np.frexp(amax)[1] - 1 + 127, 0) - down, 1)
    scale = np.exp2(byte - 127.0)
    codes = (blocks / scale).astype(np.float32).astype(dtype).astype(np.float64)
    return np.moveaxis((codes * scale).reshape(v.shape), -1, axis)


WIDE = False


def mx_kscale(k):
    if not WIDE:
        return np.ones(k)
    levels = np.array([10, -10, 5, -5, 0])
    if k % 512:
        return np.exp2(np.random.permutation(np.resize(levels, k // 32))).repeat(32)
    a = np.empty((k // 512, 16))
    for p in range(k // 512):
        a[p, :8] = np.random.permutation(np.resize(levels, 8))
        for g in range(8):
            far = levels[np.abs(levels - a[p, g]) >= 10]
            a[p, g + 8] = far[np.random.randint(len(far))]
    return np.exp2(a.ravel()).repeat(32)


BF16 = ml_dtypes.bfloat16


def bf(x):
    return np.asarray(x, np.float32).astype(BF16)


def f64(x):
    return np.asarray(x).astype(np.float64)


B, T, C, CO, HS, DW, DA, DV, DG = 4, 128, 2048, 2048, 64, 128, 128, 128, 256
H = CO // HS
EPS_NORM = 1e-12


def sigmoid(u):
    return 1.0 / (1.0 + np.exp(-u))


def setup_inputs():
    n = np.random.standard_normal
    s = mx_kscale(C)
    return {
        "x": bf(n((B, T, C)) * s),
        "x_k": bf(n((1, 1, C)) * 0.3),
        "W_k": bf(n((CO, C)) / np.sqrt(C) / s),
        "a_hid": bf(n((B, T, DA))),
        "a2": bf(n((DA, CO)) / np.sqrt(DA)),
        "a0": bf(n((1, 1, CO)) * 0.5),
        "k_k": bf(0.71 + n((1, 1, CO)) * 0.2),
        "k_a": bf(1.02 + n((1, 1, CO)) * 0.2),
    }


def reference(x, x_k, W_k, a_hid, a2, a0, k_k, k_a):
    x = f64(x)
    prev = np.concatenate([np.zeros_like(x[:, :1]), x[:, :-1]], axis=1)
    xk = x + (prev - x) * f64(x_k)
    k = mxq(xk, 2, "e4m3") @ mxq(f64(W_k), 1, "e4m3").T
    a = sigmoid(f64(a0) + f64(a_hid) @ f64(a2))
    kkh = (k * f64(k_k)).reshape(B, T, H, HS)
    nrm = np.sqrt(np.sum(kkh * kkh, axis=-1, keepdims=True))
    kk = (kkh / np.maximum(nrm, EPS_NORM)).reshape(B, T, CO)
    k_out = k * (1.0 + (a - 1.0) * f64(k_a))
    return k_out, kk

@@ -1,0 +1,302 @@
+from contextlib import ExitStack
+
+import concourse.mybir as mybir
+from concourse.masks import make_identity
+
+BF16 = mybir.dt.bfloat16
+F32 = mybir.dt.float32
+U32 = mybir.dt.uint32
+U8 = mybir.dt.uint8
+FP8X4 = mybir.dt.float8_e4m3fn_x4
+ACT = mybir.ActivationFunctionType
+ALU = mybir.AluOpType
+
+P = 128
+SEQS = 4
+T = 128
+TOKENS = SEQS * T
+C = 2048
+CO = 2048
+DA = 128
+HEAD = 64
+PACK = 4
+K_PASS = P * PACK
+PASSES = C // K_PASS
+WORDS = K_PASS // 2
+N_TILE = 512
+N_TILES = CO // N_TILE
+BLOCKS = N_TILE // P
+HEADS = N_TILE // HEAD
+BANK_WORDS = 512
+BANKS = 8
+UNITS = N_TILES * PASSES
+AHEAD = 1
+STEPS = N_TILES * SEQS
+NORM_FLOOR = 1e-12
+
+FLOPS = 2 * TOKENS * C * CO + 2 * TOKENS * DA * CO
+
+
+def tile_full_tmix_params_pa_kernel(tc, x, x_k, W_k, a_hid, a2, a0, k_k, k_a, out_0, out_1):
+    nc = tc.nc
+    with ExitStack() as ctx:
+        ctx.enter_context(tc.manual_schedule())
+        keep = ctx.enter_context(tc.tile_pool(name="keep", bufs=1))
+        x_pool = ctx.enter_context(tc.tile_pool(name="x_pool", bufs=PASSES))
+        w_pool = ctx.enter_context(tc.tile_pool(name="w_pool", bufs=CO // P))
+        stage = ctx.enter_context(tc.tile_pool(name="stage", bufs=2))
+        wq_pool = ctx.enter_context(tc.tile_pool(name="wq_pool", bufs=2 * PASSES + AHEAD))
+        gate_t_pool = ctx.enter_context(tc.tile_pool(name="gate_t_pool", bufs=CO // P))
+        gate_pool = ctx.enter_context(tc.tile_pool(name="gate_pool", bufs=3))
+        tail = ctx.enter_context(tc.tile_pool(name="tail", bufs=3))
+
+        warm = keep.tile([P, 2], F32)
+        nc.vector.memset(warm[:], 0.0)
+        nc.scalar.activation(out=warm[:, 1:2], in_=warm[:, 0:1], func=ACT.Sigmoid)
+
+        ident_bf = keep.tile([P, P], BF16)
+        make_identity(nc, ident_bf[:])
+        ident_f32 = keep.tile([P, P], F32)
+        make_identity(nc, ident_f32[:])
+
+        mix_rows = keep.tile([P, K_PASS], BF16)
+        nc.vector.memset(mix_rows[:], 0.0)
+        gate_rows = keep.tile([P, P], BF16)
+        nc.vector.memset(gate_rows[:], 0.0)
+        hid = keep.tile([P, SEQS, DA], BF16)
+        a2_sb = keep.tile([DA, CO], BF16)
+        k_k_all = keep.tile([P, CO], BF16)
+
+        nc.sync.dma_start(out=mix_rows[0:PASSES, :], in_=x_k.rearrange("a b (r c) -> (a b r) c", c=K_PASS))
+        x_tiles = []
+        for g in range(PASSES):
+            x_g = x_pool.tile([P, SEQS, K_PASS], BF16, name="x_g")
+            nc.sync.dma_start(out=x_g[:], in_=x[:, :, g * K_PASS : (g + 1) * K_PASS].rearrange("b t c -> t b c"))
+            x_tiles.append(x_g)
+            if g == 0:
+                nc.sync.dma_start(out=hid[:], in_=a_hid.rearrange("b t d -> t b d"))
+                nc.sync.dma_start(out=a2_sb[:], in_=a2)
+                nc.sync.dma_start(out=gate_rows[0 : CO // P, :], in_=a0.rearrange("a b (j p) -> (a b j) p", p=P))
+                nc.sync.dma_start(
+                    out=gate_rows[CO // P : 2 * CO // P, :], in_=k_a.rearrange("a b (j p) -> (a b j) p", p=P)
+                )
+        w_tiles = []
+        for i in range(CO // P):
+            w_i = w_pool.tile([P, C], BF16, name="w_i")
+            nc.sync.dma_start(out=w_i[:], in_=W_k[i * P : (i + 1) * P, :])
+            w_tiles.append(w_i)
+            if i == BLOCKS - 1:
+                nc.sync.dma_start(out=k_k_all[:], in_=k_k.rearrange("a b c -> (a b c)").partition_broadcast(P))
+
+        mix = keep.tile([P, PACK, PASSES], F32)
+        stay = keep.tile([P, PACK, PASSES], F32)
+        neg = keep.tile([P, 2 * CO // P], F32)
+        hid_t = keep.tile([DA, TOKENS], BF16)
+        xk_codes = keep.tile([P, PASSES, TOKENS], U32, align_bytes=64)
+        xk_scales = keep.tile([P, PASSES, TOKENS], U8, align_bytes=64)
+        shifted_ring = [keep.tile([P, SEQS, T], F32, name="shifted%d" % i) for i in range(3)]
+        for shifted in shifted_ring:
+            nc.vector.memset(shifted[:, :, 0:1], 0.0)
+
+        def mix_channels(banks, g, t, planes):
+            x_t = banks.tile([P, TOKENS], BF16, tag="bank")
+            for b in range(SEQS):
+                nc.tensor.transpose(
+                    x_t[:, b * T : (b + 1) * T], x_tiles[g][:, b, t:K_PASS:PACK], ident_bf[:]
+                )
+            shifted = shifted_ring[(g * PACK + t) % len(shifted_ring)]
+            nc.scalar.activation(
+                out=shifted[:, :, 1:T],
+                in_=x_t[:].rearrange("p (b r) -> p b r", b=SEQS)[:, :, 0 : T - 1],
+                func=ACT.Copy,
+                scale=mix[:, t, g : g + 1],
+            )
+            nc.vector.scalar_tensor_tensor(
+                out=planes[:, t, :],
+                in0=x_t[:],
+                scalar=stay[:, t, g : g + 1],
+                in1=shifted[:].rearrange("p b r -> p (b r)"),
+                op0=ALU.mult,
+                op1=ALU.add,
+            )
+
+        def regroup_tokens(planes):
+            grouped = stage.tile([P, TOKENS * PACK], BF16, align_bytes=64)
+            nc.vector.tensor_copy(
+                out=grouped[:].rearrange("p (c i t) -> p c t i", i=4, t=PACK),
+                in_=planes[:].rearrange("p t (c i) -> p c t i", i=4),
+            )
+            return grouped
+
+        def quantise_tokens(g, grouped):
+            nc.vector.quantize_mx(out=xk_codes[:, g, :].bitcast(FP8X4), scales=xk_scales[:, g, :], in_=grouped[:])
+
+        def regroup_weights(banks, unit):
+            n, g = divmod(unit, PASSES)
+            w_grouped = stage.tile([P, N_TILE * PACK], BF16, align_bytes=64, bufs=3)
+            words = w_grouped[:].bitcast(F32)
+            for h in range(BLOCKS // 2):
+                w_t = banks.tile([P, 2, 2 * P], F32, tag="bank")
+                for u in range(2):
+                    for i in range(2):
+                        nc.tensor.transpose(
+                            w_t[:, u, i * P : (i + 1) * P],
+                            w_tiles[n * BLOCKS + 2 * h + i][:].bitcast(F32)[:, g * WORDS + u : (g + 1) * WORDS : 2],
+                            ident_f32[:],
+                        )
+                nc.scalar.copy(
+                    out=words[:, h * BANK_WORDS : (h + 1) * BANK_WORDS].rearrange("p (c u) -> p c u", u=2),
+                    in_=w_t[:].rearrange("p u c -> p c u"),
+                )
+            return w_grouped
+
+        def quantise_weights(w_grouped):
+            w_codes = wq_pool.tile([P, N_TILE], U32, align_bytes=64)
+            w_scales = wq_pool.tile([P, N_TILE], U8, align_bytes=64)
+            nc.vector.quantize_mx(out=w_codes[:].bitcast(FP8X4), scales=w_scales[:], in_=w_grouped[:])
+            return w_codes, w_scales
+
+        def gate_by_channel(banks, j):
+            z_ps = banks.tile([P, TOKENS], F32, tag="bank")
+            nc.tensor.matmul(z_ps[:], lhsT=a2_sb[:, j * P : (j + 1) * P], rhs=hid_t[:], start=True, stop=True)
+            gate_t = gate_t_pool.tile([P, TOKENS], F32)
+            nc.scalar.activation(out=gate_t[:], in_=z_ps[:], func=ACT.Sigmoid, scale=-1.0, bias=neg[:, j : j + 1])
+            nc.gpsimd.tensor_scalar(
+                out=gate_t[:],
+                in0=gate_t[:],
+                scalar1=neg[:, CO // P + j : CO // P + j + 1],
+                scalar2=1.0,
+                op0=ALU.mult,
+                op1=ALU.add,
+            )
+            return gate_t
+
+        def gate_by_token(banks, n, b):
+            g_ps = banks.tile([P, N_TILE], F32, tag="bank")
+            for i in range(BLOCKS):
+                nc.tensor.transpose(
+                    g_ps[:, i * P : (i + 1) * P], gate_ts[n * BLOCKS + i][:, b * T : (b + 1) * T], ident_f32[:]
+                )
+            gate = gate_pool.tile([P, N_TILE], F32)
+            nc.scalar.copy(out=gate[:], in_=g_ps[:])
+            return gate
+
+        def multiply(sums, n, b):
+            k_ps = sums.tile([P, N_TILE], F32)
+            for g in range(PASSES):
+                w_codes, w_scales = quantised[n * PASSES + g]
+                nc.tensor.matmul_mx(
+                    out=k_ps[:],
+                    lhsT=xk_codes[:, g, b * T : (b + 1) * T].bitcast(FP8X4),
+                    lhsT_scale=xk_scales[:, g, b * T : (b + 1) * T],
+                    rhs=w_codes[:].bitcast(FP8X4),
+                    rhs_scale=w_scales[:],
+                    start=(g == 0),
+                    stop=(g == PASSES - 1),
+                )
+            return k_ps
+
+        def scale_by_k_k(n, k_ps):
+            scaled = tail.tile([P, N_TILE], F32, bufs=4)
+            nc.vector.tensor_tensor(
+                out=scaled[:], in0=k_ps[:], in1=k_k_all[:, n * N_TILE : (n + 1) * N_TILE], op=ALU.mult
+            )
+            squares = tail.tile([P, N_TILE], F32, bufs=2)
+            nc.scalar.activation(out=squares[:], in_=scaled[:], func=ACT.Square)
+            return scaled, squares
+
+        def store_k_out(n, b, k_ps, gate):
+            k_out = tail.tile([P, N_TILE], F32)
+            nc.vector.tensor_tensor(out=k_out[:], in0=k_ps[:], in1=gate[:], op=ALU.mult)
+            nc.sync.dma_start(out=out_0[b, :, n * N_TILE : (n + 1) * N_TILE], in_=k_out[:])
+
+        def sum_squares(squares):
+            sum_sq = tail.tile([P, HEADS], F32)
+            nc.vector.tensor_reduce(
+                out=sum_sq[:], in_=squares[:].rearrange("p (h d) -> p h d", d=HEAD), axis=mybir.AxisListType.X, op=ALU.add
+            )
+            return sum_sq
+
+        def floor_sums(sum_sq):
+            nc.vector.tensor_scalar_max(out=sum_sq[:], in0=sum_sq[:], scalar1=NORM_FLOOR * NORM_FLOOR)
+
+        def store_kk(n, b, scaled, sum_sq, multiplier):
+            inv_sq = tail.tile([P, HEADS], F32)
+            nc.vector.reciprocal(out=inv_sq[:], in_=sum_sq[:])
+            inv_norm = tail.tile([P, HEADS], F32)
+            nc.scalar.sqrt(out=inv_norm[:], in_=inv_sq[:])
+            kk = tail.tile([P, N_TILE], F32)
+            multiplier.tensor_tensor(
+                out=kk[:].rearrange("p (h d) -> p h d", d=HEAD),
+                in0=scaled[:].rearrange("p (h d) -> p h d", d=HEAD),
+                in1=inv_norm[:].unsqueeze(2).to_broadcast([P, HEADS, HEAD]),
+                op=ALU.mult,
+            )
+            nc.sync.dma_start(out=out_1[b, :, n * N_TILE : (n + 1) * N_TILE], in_=kk[:])
+
+        gate_ts = []
+        quantised = []
+        gates = {}
+
+        with tc.psum_pool(name="early", bufs=BANKS) as early:
+            mix_ps = early.tile([P, PACK, P], BF16, tag="bank")
+            for t in range(PACK):
+                nc.tensor.transpose(mix_ps[:, t, :], mix_rows[:, t:K_PASS:PACK], ident_bf[:])
+            nc.vector.tensor_copy(out=mix[:], in_=mix_ps[:, :, 0:PASSES])
+            nc.vector.tensor_scalar(
+                out=stay[:], in0=mix_ps[:, :, 0:PASSES], scalar1=-1.0, scalar2=1.0, op0=ALU.mult, op1=ALU.add
+            )
+            for g in range(PASSES):
+                mixed = planes if g > 0 else None
+                planes = stage.tile([P, PACK, TOKENS], BF16)
+                for t in range(PACK):
+                    mix_channels(early, g, t, planes)
+                    if g > 0:
+                        gate_ts.append(gate_by_channel(early, len(gate_ts)))
+                    if g > 0 and t == 0:
+                        grouped = regroup_tokens(mixed)
+                    if g > 0 and t == 1:
+                        quantise_tokens(g - 1, grouped)
+                if g == 0:
+                    neg_ps = early.tile([P, P], BF16, tag="bank")
+                    nc.tensor.transpose(neg_ps[:], gate_rows[:], ident_bf[:])
+                    nc.vector.tensor_scalar(
+                        out=neg[:], in0=neg_ps[:, 0 : 2 * CO // P], scalar1=-1.0, scalar2=None, op0=ALU.mult
+                    )
+                    hid_ps = early.tile([P, TOKENS], BF16, tag="bank")
+                    for b in range(SEQS):
+                        nc.tensor.transpose(hid_ps[:, b * T : (b + 1) * T], hid[:, b, :], ident_bf[:])
+                    nc.vector.tensor_copy(out=hid_t[:], in_=hid_ps[:])
+            quantise_tokens(PASSES - 1, regroup_tokens(planes))
+            for unit in range(PASSES + AHEAD):
+                quantised.append(quantise_weights(regroup_weights(early, unit)))
+                if len(gate_ts) < CO // P:
+                    gate_ts.append(gate_by_channel(early, len(gate_ts)))
+            gates[0] = gate_by_token(early, 0, 0)
+
+        with tc.psum_pool(name="work", bufs=BANKS - SEQS, reuse_waits="tile") as work, tc.psum_pool(
+            name="sums", bufs=SEQS, reuse_waits="tile"
+        ) as sums:
+            before = None
+            for step in range(STEPS):
+                n, b = divmod(step, SEQS)
+                k_ps = multiply(sums, n, b)
+                unit = len(quantised)
+                if unit < UNITS:
+                    w_grouped = regroup_weights(work, unit)
+                if step + 1 < STEPS:
+                    gates[step + 1] = gate_by_token(work, *divmod(step + 1, SEQS))
+                if before is not None:
+                    sum_sq = sum_squares(before[3])
+                scaled, squares = scale_by_k_k(n, k_ps)
+                if before is not None:
+                    floor_sums(sum_sq)
+                store_k_out(n, b, k_ps, gates[step])
+                if before is not None:
+                    store_kk(before[0], before[1], before[2], sum_sq, nc.gpsimd)
+                if unit < UNITS:
+                    quantised.append(quantise_weights(w_grouped))
+                before = (n, b, scaled, squares)
+            sum_sq = sum_squares(before[3])
+            floor_sums(sum_sq)
+            store_kk(before[0], before[1], before[2], sum_sq, nc.vector)

@@ -30,7 +30,9 @@ HEADS = N_TILE // HEAD
 BANK_WORDS = 512
 BANKS = 8
 UNITS = N_TILES * PASSES
-AHEAD = 1
+EARLY_UNITS = 5
+EARLY_GATES = 12
+ACCUM_FROM = 10
 STEPS = N_TILES * SEQS
 NORM_FLOOR = 1e-12
 
@@ -45,9 +47,8 @@ def tile_full_tmix_params_pa_kernel(tc, x, x_k, W_k, a_hid, a2, a0, k_k, k_a, ou
         x_pool = ctx.enter_context(tc.tile_pool(name="x_pool", bufs=PASSES))
         w_pool = ctx.enter_context(tc.tile_pool(name="w_pool", bufs=CO // P))
         stage = ctx.enter_context(tc.tile_pool(name="stage", bufs=2))
-        wq_pool = ctx.enter_context(tc.tile_pool(name="wq_pool", bufs=2 * PASSES + AHEAD))
-        gate_t_pool = ctx.enter_context(tc.tile_pool(name="gate_t_pool", bufs=CO // P))
-        gate_pool = ctx.enter_context(tc.tile_pool(name="gate_pool", bufs=3))
+        wq_pool = ctx.enter_context(tc.tile_pool(name="wq_pool", bufs=2 * PASSES + 2))
+        gate_pool = ctx.enter_context(tc.tile_pool(name="gate_pool", bufs=STEPS))
         tail = ctx.enter_context(tc.tile_pool(name="tail", bufs=3))
 
         warm = keep.tile([P, 2], F32)
@@ -61,11 +62,12 @@ def tile_full_tmix_params_pa_kernel(tc, x, x_k, W_k, a_hid, a2, a0, k_k, k_a, ou
 
         mix_rows = keep.tile([P, K_PASS], BF16)
         nc.vector.memset(mix_rows[:], 0.0)
-        gate_rows = keep.tile([P, P], BF16)
-        nc.vector.memset(gate_rows[:], 0.0)
+        a0_rows = keep.tile([P, P], BF16)
+        nc.vector.memset(a0_rows[:], 0.0)
         hid = keep.tile([P, SEQS, DA], BF16)
         a2_sb = keep.tile([DA, CO], BF16)
         k_k_all = keep.tile([P, CO], BF16)
+        neg_k_a = keep.tile([P, CO], BF16)
 
         nc.sync.dma_start(out=mix_rows[0:PASSES, :], in_=x_k.rearrange("a b (r c) -> (a b r) c", c=K_PASS))
         x_tiles = []
@@ -73,13 +75,11 @@ def tile_full_tmix_params_pa_kernel(tc, x, x_k, W_k, a_hid, a2, a0, k_k, k_a, ou
             x_g = x_pool.tile([P, SEQS, K_PASS], BF16, name="x_g")
             nc.sync.dma_start(out=x_g[:], in_=x[:, :, g * K_PASS : (g + 1) * K_PASS].rearrange("b t c -> t b c"))
             x_tiles.append(x_g)
-            if g == 0:
+            if g == 1:
+                nc.sync.dma_start(out=a0_rows[0 : CO // P, :], in_=a0.rearrange("a b (j p) -> (a b j) p", p=P))
                 nc.sync.dma_start(out=hid[:], in_=a_hid.rearrange("b t d -> t b d"))
                 nc.sync.dma_start(out=a2_sb[:], in_=a2)
-                nc.sync.dma_start(out=gate_rows[0 : CO // P, :], in_=a0.rearrange("a b (j p) -> (a b j) p", p=P))
-                nc.sync.dma_start(
-                    out=gate_rows[CO // P : 2 * CO // P, :], in_=k_a.rearrange("a b (j p) -> (a b j) p", p=P)
-                )
+                nc.sync.dma_start(out=neg_k_a[:], in_=k_a.rearrange("a b c -> (a b c)").partition_broadcast(P))
         w_tiles = []
         for i in range(CO // P):
             w_i = w_pool.tile([P, C], BF16, name="w_i")
@@ -90,7 +90,7 @@ def tile_full_tmix_params_pa_kernel(tc, x, x_k, W_k, a_hid, a2, a0, k_k, k_a, ou
 
         mix = keep.tile([P, PACK, PASSES], F32)
         stay = keep.tile([P, PACK, PASSES], F32)
-        neg = keep.tile([P, 2 * CO // P], F32)
+        a0_cols = keep.tile([P, CO // P], F32)
         hid_t = keep.tile([DA, TOKENS], BF16)
         xk_codes = keep.tile([P, PASSES, TOKENS], U32, align_bytes=64)
         xk_scales = keep.tile([P, PASSES, TOKENS], U8, align_bytes=64)
@@ -101,9 +101,7 @@ def tile_full_tmix_params_pa_kernel(tc, x, x_k, W_k, a_hid, a2, a0, k_k, k_a, ou
         def mix_channels(banks, g, t, planes):
             x_t = banks.tile([P, TOKENS], BF16, tag="bank")
             for b in range(SEQS):
-                nc.tensor.transpose(
-                    x_t[:, b * T : (b + 1) * T], x_tiles[g][:, b, t:K_PASS:PACK], ident_bf[:]
-                )
+                nc.tensor.transpose(x_t[:, b * T : (b + 1) * T], x_tiles[g][:, b, t:K_PASS:PACK], ident_bf[:])
             shifted = shifted_ring[(g * PACK + t) % len(shifted_ring)]
             nc.scalar.activation(
                 out=shifted[:, :, 1:T],
@@ -154,32 +152,34 @@ def tile_full_tmix_params_pa_kernel(tc, x, x_k, W_k, a_hid, a2, a0, k_k, k_a, ou
             w_codes = wq_pool.tile([P, N_TILE], U32, align_bytes=64)
             w_scales = wq_pool.tile([P, N_TILE], U8, align_bytes=64)
             nc.vector.quantize_mx(out=w_codes[:].bitcast(FP8X4), scales=w_scales[:], in_=w_grouped[:])
-            return w_codes, w_scales
+            quantised.append((w_codes, w_scales))
 
-        def gate_by_channel(banks, j):
-            z_ps = banks.tile([P, TOKENS], F32, tag="bank")
-            nc.tensor.matmul(z_ps[:], lhsT=a2_sb[:, j * P : (j + 1) * P], rhs=hid_t[:], start=True, stop=True)
-            gate_t = gate_t_pool.tile([P, TOKENS], F32)
-            nc.scalar.activation(out=gate_t[:], in_=z_ps[:], func=ACT.Sigmoid, scale=-1.0, bias=neg[:, j : j + 1])
-            nc.gpsimd.tensor_scalar(
-                out=gate_t[:],
-                in0=gate_t[:],
-                scalar1=neg[:, CO // P + j : CO // P + j + 1],
-                scalar2=1.0,
-                op0=ALU.mult,
-                op1=ALU.add,
+        def make_gate(banks):
+            n, b = divmod(len(gates), SEQS)
+            z_ps = banks.tile([P, N_TILE], F32, tag="bank")
+            nc.tensor.matmul(
+                z_ps[:],
+                lhsT=hid_t[:, b * T : (b + 1) * T],
+                rhs=a2_sb[:, n * N_TILE : (n + 1) * N_TILE],
+                start=True,
+                stop=False,
             )
-            return gate_t
-
-        def gate_by_token(banks, n, b):
-            g_ps = banks.tile([P, N_TILE], F32, tag="bank")
             for i in range(BLOCKS):
-                nc.tensor.transpose(
-                    g_ps[:, i * P : (i + 1) * P], gate_ts[n * BLOCKS + i][:, b * T : (b + 1) * T], ident_f32[:]
+                j = n * BLOCKS + i
+                nc.tensor.matmul(
+                    z_ps[:, i * P : (i + 1) * P],
+                    lhsT=a0_cols[:, j : j + 1].to_broadcast([P, P]),
+                    rhs=ident_f32[:],
+                    is_transpose=True,
+                    start=False,
+                    stop=(i == BLOCKS - 1),
                 )
             gate = gate_pool.tile([P, N_TILE], F32)
-            nc.scalar.copy(out=gate[:], in_=g_ps[:])
-            return gate
+            nc.scalar.activation(out=gate[:], in_=z_ps[:], func=ACT.Sigmoid, scale=-1.0)
+            nc.gpsimd.tensor_tensor(
+                out=gate[:], in0=gate[:], in1=neg_k_a[:, n * N_TILE : (n + 1) * N_TILE], op=ALU.mult
+            )
+            gates.append(gate)
 
         def multiply(sums, n, b):
             k_ps = sums.tile([P, N_TILE], F32)
@@ -197,25 +197,42 @@ def tile_full_tmix_params_pa_kernel(tc, x, x_k, W_k, a_hid, a2, a0, k_k, k_a, ou
             return k_ps
 
         def scale_by_k_k(n, k_ps):
-            scaled = tail.tile([P, N_TILE], F32, bufs=4)
+            scaled = tail.tile([P, N_TILE], F32, bufs=6)
             nc.vector.tensor_tensor(
                 out=scaled[:], in0=k_ps[:], in1=k_k_all[:, n * N_TILE : (n + 1) * N_TILE], op=ALU.mult
             )
+            return scaled
+
+        def square(scaled):
             squares = tail.tile([P, N_TILE], F32, bufs=2)
             nc.scalar.activation(out=squares[:], in_=scaled[:], func=ACT.Square)
-            return scaled, squares
+            return squares
 
-        def store_k_out(n, b, k_ps, gate):
-            k_out = tail.tile([P, N_TILE], F32)
-            nc.vector.tensor_tensor(out=k_out[:], in0=k_ps[:], in1=gate[:], op=ALU.mult)
-            nc.sync.dma_start(out=out_0[b, :, n * N_TILE : (n + 1) * N_TILE], in_=k_out[:])
-
-        def sum_squares(squares):
+        def sum_squares_on_vector(squares):
             sum_sq = tail.tile([P, HEADS], F32)
             nc.vector.tensor_reduce(
                 out=sum_sq[:], in_=squares[:].rearrange("p (h d) -> p h d", d=HEAD), axis=mybir.AxisListType.X, op=ALU.add
             )
             return sum_sq
+
+        def sum_squares_on_scalar(scaled):
+            sum_sq = tail.tile([P, HEADS], F32)
+            squares = tail.tile([P, N_TILE], F32, bufs=2)
+            for h in range(HEADS):
+                nc.scalar.activation(
+                    out=squares[:, h * HEAD : (h + 1) * HEAD],
+                    in_=scaled[:, h * HEAD : (h + 1) * HEAD],
+                    func=ACT.Square,
+                    accum_out=sum_sq[:, h : h + 1],
+                )
+            return sum_sq
+
+        def store_k_out(n, b, k_ps, gate):
+            k_out = tail.tile([P, N_TILE], F32)
+            nc.vector.scalar_tensor_tensor(
+                out=k_out[:], in0=gate[:], scalar=1.0, in1=k_ps[:], op0=ALU.add, op1=ALU.mult
+            )
+            nc.sync.dma_start(out=out_0[b, :, n * N_TILE : (n + 1) * N_TILE], in_=k_out[:])
 
         def floor_sums(sum_sq):
             nc.vector.tensor_scalar_max(out=sum_sq[:], in0=sum_sq[:], scalar1=NORM_FLOOR * NORM_FLOOR)
@@ -234,9 +251,8 @@ def tile_full_tmix_params_pa_kernel(tc, x, x_k, W_k, a_hid, a2, a0, k_k, k_a, ou
             )
             nc.sync.dma_start(out=out_1[b, :, n * N_TILE : (n + 1) * N_TILE], in_=kk[:])
 
-        gate_ts = []
         quantised = []
-        gates = {}
+        gates = []
 
         with tc.psum_pool(name="early", bufs=BANKS) as early:
             mix_ps = early.tile([P, PACK, P], BF16, tag="bank")
@@ -252,51 +268,57 @@ def tile_full_tmix_params_pa_kernel(tc, x, x_k, W_k, a_hid, a2, a0, k_k, k_a, ou
                 for t in range(PACK):
                     mix_channels(early, g, t, planes)
                     if g > 0:
-                        gate_ts.append(gate_by_channel(early, len(gate_ts)))
+                        make_gate(early)
                     if g > 0 and t == 0:
                         grouped = regroup_tokens(mixed)
                     if g > 0 and t == 1:
                         quantise_tokens(g - 1, grouped)
                 if g == 0:
-                    neg_ps = early.tile([P, P], BF16, tag="bank")
-                    nc.tensor.transpose(neg_ps[:], gate_rows[:], ident_bf[:])
-                    nc.vector.tensor_scalar(
-                        out=neg[:], in0=neg_ps[:, 0 : 2 * CO // P], scalar1=-1.0, scalar2=None, op0=ALU.mult
-                    )
+                    a0_ps = early.tile([P, P], BF16, tag="bank")
+                    nc.tensor.transpose(a0_ps[:], a0_rows[:], ident_bf[:])
+                    nc.scalar.copy(out=a0_cols[:], in_=a0_ps[:, 0 : CO // P])
                     hid_ps = early.tile([P, TOKENS], BF16, tag="bank")
                     for b in range(SEQS):
                         nc.tensor.transpose(hid_ps[:, b * T : (b + 1) * T], hid[:, b, :], ident_bf[:])
-                    nc.vector.tensor_copy(out=hid_t[:], in_=hid_ps[:])
-            quantise_tokens(PASSES - 1, regroup_tokens(planes))
-            for unit in range(PASSES + AHEAD):
-                quantised.append(quantise_weights(regroup_weights(early, unit)))
-                if len(gate_ts) < CO // P:
-                    gate_ts.append(gate_by_channel(early, len(gate_ts)))
-            gates[0] = gate_by_token(early, 0, 0)
+                    nc.scalar.copy(out=hid_t[:], in_=hid_ps[:])
+                    nc.gpsimd.tensor_scalar(
+                        out=neg_k_a[:], in0=neg_k_a[:], scalar1=-1.0, scalar2=0.0, op0=ALU.mult, op1=ALU.add
+                    )
+            w_grouped = regroup_weights(early, 0)
+            grouped = regroup_tokens(planes)
+            quantise_weights(w_grouped)
+            quantise_tokens(PASSES - 1, grouped)
+            for unit in range(1, EARLY_UNITS):
+                quantise_weights(regroup_weights(early, unit))
 
-        with tc.psum_pool(name="work", bufs=BANKS - SEQS, reuse_waits="tile") as work, tc.psum_pool(
-            name="sums", bufs=SEQS, reuse_waits="tile"
+        with tc.psum_pool(name="work", bufs=5, reuse_waits="tile") as work, tc.psum_pool(
+            name="sums", bufs=3, reuse_waits="tile"
         ) as sums:
             before = None
+            w_grouped = None
             for step in range(STEPS):
                 n, b = divmod(step, SEQS)
                 k_ps = multiply(sums, n, b)
-                unit = len(quantised)
-                if unit < UNITS:
-                    w_grouped = regroup_weights(work, unit)
-                if step + 1 < STEPS:
-                    gates[step + 1] = gate_by_token(work, *divmod(step + 1, SEQS))
-                if before is not None:
-                    sum_sq = sum_squares(before[3])
-                scaled, squares = scale_by_k_k(n, k_ps)
+                w_ready = w_grouped
+                unit = EARLY_UNITS + step
+                w_grouped = regroup_weights(work, unit) if unit < UNITS else None
+                for i in range(2):
+                    if len(gates) < STEPS:
+                        make_gate(work)
+                if before is not None and step <= ACCUM_FROM:
+                    sum_sq = sum_squares_on_vector(before[3])
+                scaled = scale_by_k_k(n, k_ps)
                 if before is not None:
                     floor_sums(sum_sq)
                 store_k_out(n, b, k_ps, gates[step])
+                if step < ACCUM_FROM:
+                    squares = square(scaled)
                 if before is not None:
-                    store_kk(before[0], before[1], before[2], sum_sq, nc.gpsimd)
-                if unit < UNITS:
-                    quantised.append(quantise_weights(w_grouped))
+                    store_kk(*before[0:3], sum_sq, nc.gpsimd)
+                if step >= ACCUM_FROM:
+                    sum_sq = sum_squares_on_scalar(scaled)
+                if w_ready is not None:
+                    quantise_weights(w_ready)
                 before = (n, b, scaled, squares)
-            sum_sq = sum_squares(before[3])
             floor_sums(sum_sq)
-            store_kk(before[0], before[1], before[2], sum_sq, nc.vector)
+            store_kk(*before[0:3], sum_sq, nc.vector)

@@ -31,8 +31,6 @@ BANK_WORDS = 512
 BANKS = 8
 UNITS = N_TILES * PASSES
 EARLY_UNITS = 5
-EARLY_GATES = 12
-ACCUM_FROM = 10
 STEPS = N_TILES * SEQS
 NORM_FLOOR = 1e-12
 
@@ -45,7 +43,7 @@ def tile_full_tmix_params_pa_kernel(tc, x, x_k, W_k, a_hid, a2, a0, k_k, k_a, ou
         ctx.enter_context(tc.manual_schedule())
         keep = ctx.enter_context(tc.tile_pool(name="keep", bufs=1))
         x_pool = ctx.enter_context(tc.tile_pool(name="x_pool", bufs=PASSES))
-        w_pool = ctx.enter_context(tc.tile_pool(name="w_pool", bufs=CO // P))
+        w_pool = ctx.enter_context(tc.tile_pool(name="w_pool", bufs=12))
         stage = ctx.enter_context(tc.tile_pool(name="stage", bufs=2))
         wq_pool = ctx.enter_context(tc.tile_pool(name="wq_pool", bufs=2 * PASSES + 2))
         gate_pool = ctx.enter_context(tc.tile_pool(name="gate_pool", bufs=STEPS))
@@ -70,16 +68,16 @@ def tile_full_tmix_params_pa_kernel(tc, x, x_k, W_k, a_hid, a2, a0, k_k, k_a, ou
         neg_k_a = keep.tile([P, CO], BF16)
 
         nc.sync.dma_start(out=mix_rows[0:PASSES, :], in_=x_k.rearrange("a b (r c) -> (a b r) c", c=K_PASS))
+        nc.sync.dma_start(out=a0_rows[0 : CO // P, :], in_=a0.rearrange("a b (j p) -> (a b j) p", p=P))
         x_tiles = []
         for g in range(PASSES):
             x_g = x_pool.tile([P, SEQS, K_PASS], BF16, name="x_g")
             nc.sync.dma_start(out=x_g[:], in_=x[:, :, g * K_PASS : (g + 1) * K_PASS].rearrange("b t c -> t b c"))
             x_tiles.append(x_g)
-            if g == 1:
-                nc.sync.dma_start(out=a0_rows[0 : CO // P, :], in_=a0.rearrange("a b (j p) -> (a b j) p", p=P))
+            if g == 0:
                 nc.sync.dma_start(out=hid[:], in_=a_hid.rearrange("b t d -> t b d"))
                 nc.sync.dma_start(out=a2_sb[:], in_=a2)
-                nc.sync.dma_start(out=neg_k_a[:], in_=k_a.rearrange("a b c -> (a b c)").partition_broadcast(P))
+        nc.sync.dma_start(out=neg_k_a[:], in_=k_a.rearrange("a b c -> (a b c)").partition_broadcast(P))
         w_tiles = []
         for i in range(CO // P):
             w_i = w_pool.tile([P, C], BF16, name="w_i")
@@ -90,7 +88,7 @@ def tile_full_tmix_params_pa_kernel(tc, x, x_k, W_k, a_hid, a2, a0, k_k, k_a, ou
 
         mix = keep.tile([P, PACK, PASSES], F32)
         stay = keep.tile([P, PACK, PASSES], F32)
-        a0_cols = keep.tile([P, CO // P], F32)
+        a0_cols = keep.tile([P, CO // P, P], F32)
         hid_t = keep.tile([DA, TOKENS], BF16)
         xk_codes = keep.tile([P, PASSES, TOKENS], U32, align_bytes=64)
         xk_scales = keep.tile([P, PASSES, TOKENS], U8, align_bytes=64)
@@ -98,20 +96,34 @@ def tile_full_tmix_params_pa_kernel(tc, x, x_k, W_k, a_hid, a2, a0, k_k, k_a, ou
         for shifted in shifted_ring:
             nc.vector.memset(shifted[:, :, 0:1], 0.0)
 
-        def mix_channels(banks, g, t, planes):
-            x_t = banks.tile([P, TOKENS], BF16, tag="bank")
+        def transpose_tokens(banks, g, u):
+            x_t = banks.tile([P, TOKENS], F32, tag="x")
             for b in range(SEQS):
-                nc.tensor.transpose(x_t[:, b * T : (b + 1) * T], x_tiles[g][:, b, t:K_PASS:PACK], ident_bf[:])
-            shifted = shifted_ring[(g * PACK + t) % len(shifted_ring)]
+                nc.tensor.transpose(
+                    x_t[:, b * T : (b + 1) * T], x_tiles[g][:, b, :].bitcast(F32)[:, u:WORDS:2], ident_f32[:]
+                )
+            return x_t
+
+        zeros = keep.tile([P, HEADS, 2], F32)
+        nc.vector.memset(zeros[:], 0.0)
+        sum_ring = [keep.tile([P, HEADS, 2], F32, name="sums%d" % i) for i in range(4)]
+        for sums_of in sum_ring:
+            nc.vector.tensor_scalar_add(out=sums_of[:], in0=zeros[:], scalar1=NORM_FLOOR * NORM_FLOOR)
+
+        def mix_channels(x_t, g, t, planes):
+            e = t % 2
+            pairs = x_t[:].bitcast(BF16)
+            shifted = shifted_ring[len(mixes) % len(shifted_ring)]
+            mixes.append((g, t))
             nc.scalar.activation(
                 out=shifted[:, :, 1:T],
-                in_=x_t[:].rearrange("p (b r) -> p b r", b=SEQS)[:, :, 0 : T - 1],
+                in_=pairs.rearrange("p (b r e) -> p b r e", b=SEQS, e=2)[:, :, 0 : T - 1, e],
                 func=ACT.Copy,
                 scale=mix[:, t, g : g + 1],
             )
             nc.vector.scalar_tensor_tensor(
                 out=planes[:, t, :],
-                in0=x_t[:],
+                in0=pairs[:, e : 2 * TOKENS : 2],
                 scalar=stay[:, t, g : g + 1],
                 in1=shifted[:].rearrange("p b r -> p (b r)"),
                 op0=ALU.mult,
@@ -129,12 +141,12 @@ def tile_full_tmix_params_pa_kernel(tc, x, x_k, W_k, a_hid, a2, a0, k_k, k_a, ou
         def quantise_tokens(g, grouped):
             nc.vector.quantize_mx(out=xk_codes[:, g, :].bitcast(FP8X4), scales=xk_scales[:, g, :], in_=grouped[:])
 
-        def regroup_weights(banks, unit):
+        def regroup_weights(banks, unit, copy):
             n, g = divmod(unit, PASSES)
-            w_grouped = stage.tile([P, N_TILE * PACK], BF16, align_bytes=64, bufs=3)
+            w_grouped = stage.tile([P, N_TILE * PACK], BF16, align_bytes=64, bufs=5)
             words = w_grouped[:].bitcast(F32)
             for h in range(BLOCKS // 2):
-                w_t = banks.tile([P, 2, 2 * P], F32, tag="bank")
+                w_t = banks.tile([P, 2, 2 * P], F32, tag="w")
                 for u in range(2):
                     for i in range(2):
                         nc.tensor.transpose(
@@ -142,7 +154,7 @@ def tile_full_tmix_params_pa_kernel(tc, x, x_k, W_k, a_hid, a2, a0, k_k, k_a, ou
                             w_tiles[n * BLOCKS + 2 * h + i][:].bitcast(F32)[:, g * WORDS + u : (g + 1) * WORDS : 2],
                             ident_f32[:],
                         )
-                nc.scalar.copy(
+                copy(
                     out=words[:, h * BANK_WORDS : (h + 1) * BANK_WORDS].rearrange("p (c u) -> p c u", u=2),
                     in_=w_t[:].rearrange("p u c -> p c u"),
                 )
@@ -154,9 +166,9 @@ def tile_full_tmix_params_pa_kernel(tc, x, x_k, W_k, a_hid, a2, a0, k_k, k_a, ou
             nc.vector.quantize_mx(out=w_codes[:].bitcast(FP8X4), scales=w_scales[:], in_=w_grouped[:])
             quantised.append((w_codes, w_scales))
 
-        def make_gate(banks):
+        def make_gate(banks, z_bufs=2):
             n, b = divmod(len(gates), SEQS)
-            z_ps = banks.tile([P, N_TILE], F32, tag="bank")
+            z_ps = banks.tile([P, N_TILE], F32, tag="z", bufs=z_bufs)
             nc.tensor.matmul(
                 z_ps[:],
                 lhsT=hid_t[:, b * T : (b + 1) * T],
@@ -168,7 +180,7 @@ def tile_full_tmix_params_pa_kernel(tc, x, x_k, W_k, a_hid, a2, a0, k_k, k_a, ou
                 j = n * BLOCKS + i
                 nc.tensor.matmul(
                     z_ps[:, i * P : (i + 1) * P],
-                    lhsT=a0_cols[:, j : j + 1].to_broadcast([P, P]),
+                    lhsT=a0_cols[:, j, :],
                     rhs=ident_f32[:],
                     is_transpose=True,
                     start=False,
@@ -176,10 +188,13 @@ def tile_full_tmix_params_pa_kernel(tc, x, x_k, W_k, a_hid, a2, a0, k_k, k_a, ou
                 )
             gate = gate_pool.tile([P, N_TILE], F32)
             nc.scalar.activation(out=gate[:], in_=z_ps[:], func=ACT.Sigmoid, scale=-1.0)
-            nc.gpsimd.tensor_tensor(
-                out=gate[:], in0=gate[:], in1=neg_k_a[:, n * N_TILE : (n + 1) * N_TILE], op=ALU.mult
-            )
             gates.append(gate)
+
+        def weigh_gate(step, multiplier):
+            n = step // SEQS
+            multiplier.tensor_tensor(
+                out=gates[step][:], in0=gates[step][:], in1=neg_k_a[:, n * N_TILE : (n + 1) * N_TILE], op=ALU.mult
+            )
 
         def multiply(sums, n, b):
             k_ps = sums.tile([P, N_TILE], F32)
@@ -203,29 +218,17 @@ def tile_full_tmix_params_pa_kernel(tc, x, x_k, W_k, a_hid, a2, a0, k_k, k_a, ou
             )
             return scaled
 
-        def square(scaled):
-            squares = tail.tile([P, N_TILE], F32, bufs=2)
-            nc.scalar.activation(out=squares[:], in_=scaled[:], func=ACT.Square)
-            return squares
-
-        def sum_squares_on_vector(squares):
-            sum_sq = tail.tile([P, HEADS], F32)
-            nc.vector.tensor_reduce(
-                out=sum_sq[:], in_=squares[:].rearrange("p (h d) -> p h d", d=HEAD), axis=mybir.AxisListType.X, op=ALU.add
-            )
-            return sum_sq
-
-        def sum_squares_on_scalar(scaled):
-            sum_sq = tail.tile([P, HEADS], F32)
+        def sum_squares_on_scalar(step, scaled):
+            sums_of = sum_ring[step % len(sum_ring)]
             squares = tail.tile([P, N_TILE], F32, bufs=2)
             for h in range(HEADS):
                 nc.scalar.activation(
                     out=squares[:, h * HEAD : (h + 1) * HEAD],
                     in_=scaled[:, h * HEAD : (h + 1) * HEAD],
                     func=ACT.Square,
-                    accum_out=sum_sq[:, h : h + 1],
+                    accum_out=sums_of[:, h, 0:1],
                 )
-            return sum_sq
+            return sums_of
 
         def store_k_out(n, b, k_ps, gate):
             k_out = tail.tile([P, N_TILE], F32)
@@ -234,12 +237,14 @@ def tile_full_tmix_params_pa_kernel(tc, x, x_k, W_k, a_hid, a2, a0, k_k, k_a, ou
             )
             nc.sync.dma_start(out=out_0[b, :, n * N_TILE : (n + 1) * N_TILE], in_=k_out[:])
 
-        def floor_sums(sum_sq):
-            nc.vector.tensor_scalar_max(out=sum_sq[:], in0=sum_sq[:], scalar1=NORM_FLOOR * NORM_FLOOR)
+        def floor_sums(sums_of):
+            floored = tail.tile([P, HEADS], F32)
+            nc.vector.tensor_reduce(out=floored[:], in_=sums_of[:], axis=mybir.AxisListType.X, op=ALU.max)
+            return floored
 
-        def store_kk(n, b, scaled, sum_sq, multiplier):
+        def store_kk(n, b, scaled, floored, multiplier):
             inv_sq = tail.tile([P, HEADS], F32)
-            nc.vector.reciprocal(out=inv_sq[:], in_=sum_sq[:])
+            nc.vector.reciprocal(out=inv_sq[:], in_=floored[:])
             inv_norm = tail.tile([P, HEADS], F32)
             nc.scalar.sqrt(out=inv_norm[:], in_=inv_sq[:])
             kk = tail.tile([P, N_TILE], F32)
@@ -253,72 +258,93 @@ def tile_full_tmix_params_pa_kernel(tc, x, x_k, W_k, a_hid, a2, a0, k_k, k_a, ou
 
         quantised = []
         gates = []
+        mixes = []
 
-        with tc.psum_pool(name="early", bufs=BANKS) as early:
-            mix_ps = early.tile([P, PACK, P], BF16, tag="bank")
+        with tc.psum_pool(name="early", bufs=3) as early:
+            mix_ps = early.tile([P, PACK, P], BF16, tag="x")
             for t in range(PACK):
                 nc.tensor.transpose(mix_ps[:, t, :], mix_rows[:, t:K_PASS:PACK], ident_bf[:])
             nc.vector.tensor_copy(out=mix[:], in_=mix_ps[:, :, 0:PASSES])
             nc.vector.tensor_scalar(
                 out=stay[:], in0=mix_ps[:, :, 0:PASSES], scalar1=-1.0, scalar2=1.0, op0=ALU.mult, op1=ALU.add
             )
+            a0_ps = early.tile([P, P], BF16, tag="z", bufs=2)
+            nc.tensor.transpose(a0_ps[:], a0_rows[:], ident_bf[:])
+            a0_one = keep.tile([P, CO // P], F32)
+            nc.scalar.copy(out=a0_one[:], in_=a0_ps[:, 0 : CO // P])
+            nc.gpsimd.tensor_scalar(
+                out=a0_cols[:],
+                in0=a0_one[:].unsqueeze(2).to_broadcast([P, CO // P, P]),
+                scalar1=1.0,
+                scalar2=0.0,
+                op0=ALU.mult,
+                op1=ALU.add,
+            )
+            planes, grouped, w_grouped = [], [], []
+            weighed = list(range(0, STEPS, 2))
             for g in range(PASSES):
-                mixed = planes if g > 0 else None
-                planes = stage.tile([P, PACK, TOKENS], BF16)
-                for t in range(PACK):
-                    mix_channels(early, g, t, planes)
-                    if g > 0:
+                halves = [transpose_tokens(early, g, u) for u in range(2)]
+                planes.append(stage.tile([P, PACK, TOKENS], BF16, name="planes"))
+                for i, t in enumerate((0, 2, 1, 3)):
+                    mix_channels(halves[t // 2], g, t, planes[g])
+                    if i == 0 and g > 0:
+                        grouped.append(regroup_tokens(planes[g - 1]))
+                    if i == 0 and g > 1:
+                        quantise_tokens(g - 2, grouped[g - 2])
+                    if g == 0 and i == 0:
+                        hid_ps = early.tile([P, TOKENS], BF16, tag="z", bufs=2)
+                        for b in range(SEQS):
+                            nc.tensor.transpose(hid_ps[:, b * T : (b + 1) * T], hid[:, b, :], ident_bf[:])
+                        nc.scalar.copy(out=hid_t[:], in_=hid_ps[:])
+                    if g > 0 or i > 0:
                         make_gate(early)
-                    if g > 0 and t == 0:
-                        grouped = regroup_tokens(mixed)
-                    if g > 0 and t == 1:
-                        quantise_tokens(g - 1, grouped)
-                if g == 0:
-                    a0_ps = early.tile([P, P], BF16, tag="bank")
-                    nc.tensor.transpose(a0_ps[:], a0_rows[:], ident_bf[:])
-                    nc.scalar.copy(out=a0_cols[:], in_=a0_ps[:, 0 : CO // P])
-                    hid_ps = early.tile([P, TOKENS], BF16, tag="bank")
-                    for b in range(SEQS):
-                        nc.tensor.transpose(hid_ps[:, b * T : (b + 1) * T], hid[:, b, :], ident_bf[:])
-                    nc.scalar.copy(out=hid_t[:], in_=hid_ps[:])
-                    nc.gpsimd.tensor_scalar(
-                        out=neg_k_a[:], in0=neg_k_a[:], scalar1=-1.0, scalar2=0.0, op0=ALU.mult, op1=ALU.add
-                    )
-            w_grouped = regroup_weights(early, 0)
-            grouped = regroup_tokens(planes)
-            quantise_weights(w_grouped)
-            quantise_tokens(PASSES - 1, grouped)
-            for unit in range(1, EARLY_UNITS):
-                quantise_weights(regroup_weights(early, unit))
+                    if g == 1 and i == 0:
+                        nc.vector.tensor_scalar(
+                            out=neg_k_a[:], in0=neg_k_a[:], scalar1=-1.0, scalar2=None, op0=ALU.mult
+                        )
+                    if g > 0 and i % 2 == 1:
+                        weigh_gate(weighed.pop(0), nc.gpsimd)
+                if g > 1:
+                    w_grouped.append(regroup_weights(early, len(w_grouped), nc.vector.tensor_copy))
+            w_grouped.append(regroup_weights(early, len(w_grouped), nc.scalar.copy))
+            quantise_tokens(PASSES - 2, grouped[PASSES - 2])
+            grouped.append(regroup_tokens(planes[PASSES - 1]))
+            quantise_weights(w_grouped[0])
+            quantise_tokens(PASSES - 1, grouped[PASSES - 1])
+            quantise_weights(w_grouped[1])
+            while len(w_grouped) < EARLY_UNITS:
+                w_grouped.append(regroup_weights(early, len(w_grouped), nc.scalar.copy))
+                quantise_weights(w_grouped[-2])
+                if len(gates) < STEPS:
+                    make_gate(early)
+                weigh_gate(weighed.pop(0), nc.gpsimd)
+            quantise_weights(w_grouped[-1])
 
-        with tc.psum_pool(name="work", bufs=5, reuse_waits="tile") as work, tc.psum_pool(
-            name="sums", bufs=3, reuse_waits="tile"
+        with tc.psum_pool(name="work", bufs=3, reuse_waits="tile") as work, tc.psum_pool(
+            name="sums", bufs=4, reuse_waits="tile"
         ) as sums:
-            before = None
-            w_grouped = None
+            waiting = []
             for step in range(STEPS):
                 n, b = divmod(step, SEQS)
                 k_ps = multiply(sums, n, b)
-                w_ready = w_grouped
                 unit = EARLY_UNITS + step
-                w_grouped = regroup_weights(work, unit) if unit < UNITS else None
+                if unit < UNITS:
+                    w_grouped.append(regroup_weights(work, unit, nc.scalar.copy))
+                done = waiting[:2] if len(gates) == STEPS else []
+                waiting = waiting[len(done) :]
                 for i in range(2):
                     if len(gates) < STEPS:
-                        make_gate(work)
-                if before is not None and step <= ACCUM_FROM:
-                    sum_sq = sum_squares_on_vector(before[3])
+                        make_gate(work, 1)
                 scaled = scale_by_k_k(n, k_ps)
-                if before is not None:
-                    floor_sums(sum_sq)
+                floored = [floor_sums(entry[3]) for entry in done]
                 store_k_out(n, b, k_ps, gates[step])
-                if step < ACCUM_FROM:
-                    squares = square(scaled)
-                if before is not None:
-                    store_kk(*before[0:3], sum_sq, nc.gpsimd)
-                if step >= ACCUM_FROM:
-                    sum_sq = sum_squares_on_scalar(scaled)
-                if w_ready is not None:
-                    quantise_weights(w_ready)
-                before = (n, b, scaled, squares)
-            floor_sums(sum_sq)
-            store_kk(*before[0:3], sum_sq, nc.vector)
+                sums_of = sum_squares_on_scalar(step, scaled)
+                for entry, sum_sq in zip(done, floored):
+                    store_kk(*entry[0:3], sum_sq, nc.gpsimd)
+                if step % 2 == 0:
+                    weigh_gate(step + 1, nc.vector)
+                if unit < UNITS:
+                    quantise_weights(w_grouped[unit])
+                waiting.append((n, b, scaled, sums_of))
+            for entry in waiting:
+                store_kk(*entry[0:3], floor_sums(entry[3]), nc.vector)

@@ -43,7 +43,7 @@ def tile_full_tmix_params_pa_kernel(tc, x, x_k, W_k, a_hid, a2, a0, k_k, k_a, ou
         ctx.enter_context(tc.manual_schedule())
         keep = ctx.enter_context(tc.tile_pool(name="keep", bufs=1))
         x_pool = ctx.enter_context(tc.tile_pool(name="x_pool", bufs=PASSES))
-        w_pool = ctx.enter_context(tc.tile_pool(name="w_pool", bufs=12))
+        w_pool = ctx.enter_context(tc.tile_pool(name="w_pool", bufs=10))
         stage = ctx.enter_context(tc.tile_pool(name="stage", bufs=2))
         wq_pool = ctx.enter_context(tc.tile_pool(name="wq_pool", bufs=2 * PASSES + 2))
         gate_pool = ctx.enter_context(tc.tile_pool(name="gate_pool", bufs=STEPS))
@@ -143,7 +143,7 @@ def tile_full_tmix_params_pa_kernel(tc, x, x_k, W_k, a_hid, a2, a0, k_k, k_a, ou
 
         def regroup_weights(banks, unit, copy):
             n, g = divmod(unit, PASSES)
-            w_grouped = stage.tile([P, N_TILE * PACK], BF16, align_bytes=64, bufs=5)
+            w_grouped = stage.tile([P, N_TILE * PACK], BF16, align_bytes=64, bufs=4)
             words = w_grouped[:].bitcast(F32)
             for h in range(BLOCKS // 2):
                 w_t = banks.tile([P, 2, 2 * P], F32, tag="w")
@@ -160,10 +160,10 @@ def tile_full_tmix_params_pa_kernel(tc, x, x_k, W_k, a_hid, a2, a0, k_k, k_a, ou
                 )
             return w_grouped
 
-        def quantise_weights(w_grouped):
+        def quantise_weights():
             w_codes = wq_pool.tile([P, N_TILE], U32, align_bytes=64)
             w_scales = wq_pool.tile([P, N_TILE], U8, align_bytes=64)
-            nc.vector.quantize_mx(out=w_codes[:].bitcast(FP8X4), scales=w_scales[:], in_=w_grouped[:])
+            nc.vector.quantize_mx(out=w_codes[:].bitcast(FP8X4), scales=w_scales[:], in_=w_grouped[len(quantised)][:])
             quantised.append((w_codes, w_scales))
 
         def make_gate(banks, z_bufs=2):
@@ -220,7 +220,7 @@ def tile_full_tmix_params_pa_kernel(tc, x, x_k, W_k, a_hid, a2, a0, k_k, k_a, ou
 
         def sum_squares_on_scalar(step, scaled):
             sums_of = sum_ring[step % len(sum_ring)]
-            squares = tail.tile([P, N_TILE], F32, bufs=2)
+            squares = tail.tile([P, N_TILE], F32, bufs=3)
             for h in range(HEADS):
                 nc.scalar.activation(
                     out=squares[:, h * HEAD : (h + 1) * HEAD],
@@ -231,7 +231,7 @@ def tile_full_tmix_params_pa_kernel(tc, x, x_k, W_k, a_hid, a2, a0, k_k, k_a, ou
             return sums_of
 
         def store_k_out(n, b, k_ps, gate):
-            k_out = tail.tile([P, N_TILE], F32)
+            k_out = tail.tile([P, N_TILE], F32, bufs=5)
             nc.vector.scalar_tensor_tensor(
                 out=k_out[:], in0=gate[:], scalar=1.0, in1=k_ps[:], op0=ALU.add, op1=ALU.mult
             )
@@ -242,12 +242,15 @@ def tile_full_tmix_params_pa_kernel(tc, x, x_k, W_k, a_hid, a2, a0, k_k, k_a, ou
             nc.vector.tensor_reduce(out=floored[:], in_=sums_of[:], axis=mybir.AxisListType.X, op=ALU.max)
             return floored
 
-        def store_kk(n, b, scaled, floored, multiplier):
+        def invert_sums(floored):
             inv_sq = tail.tile([P, HEADS], F32)
             nc.vector.reciprocal(out=inv_sq[:], in_=floored[:])
+            return inv_sq
+
+        def store_kk(n, b, scaled, inv_sq, multiplier):
             inv_norm = tail.tile([P, HEADS], F32)
             nc.scalar.sqrt(out=inv_norm[:], in_=inv_sq[:])
-            kk = tail.tile([P, N_TILE], F32)
+            kk = tail.tile([P, N_TILE], F32, bufs=5)
             multiplier.tensor_tensor(
                 out=kk[:].rearrange("p (h d) -> p h d", d=HEAD),
                 in0=scaled[:].rearrange("p (h d) -> p h d", d=HEAD),
@@ -256,6 +259,7 @@ def tile_full_tmix_params_pa_kernel(tc, x, x_k, W_k, a_hid, a2, a0, k_k, k_a, ou
             )
             nc.sync.dma_start(out=out_1[b, :, n * N_TILE : (n + 1) * N_TILE], in_=kk[:])
 
+        w_grouped = []
         quantised = []
         gates = []
         mixes = []
@@ -280,8 +284,8 @@ def tile_full_tmix_params_pa_kernel(tc, x, x_k, W_k, a_hid, a2, a0, k_k, k_a, ou
                 op0=ALU.mult,
                 op1=ALU.add,
             )
-            planes, grouped, w_grouped = [], [], []
-            weighed = list(range(0, STEPS, 2))
+            planes, grouped = [], []
+            weighed = list(range(STEPS))
             for g in range(PASSES):
                 halves = [transpose_tokens(early, g, u) for u in range(2)]
                 planes.append(stage.tile([P, PACK, TOKENS], BF16, name="planes"))
@@ -302,49 +306,55 @@ def tile_full_tmix_params_pa_kernel(tc, x, x_k, W_k, a_hid, a2, a0, k_k, k_a, ou
                         nc.vector.tensor_scalar(
                             out=neg_k_a[:], in0=neg_k_a[:], scalar1=-1.0, scalar2=None, op0=ALU.mult
                         )
-                    if g > 0 and i % 2 == 1:
-                        weigh_gate(weighed.pop(0), nc.gpsimd)
-                if g > 1:
-                    w_grouped.append(regroup_weights(early, len(w_grouped), nc.vector.tensor_copy))
+                    if g > 0 and i in (2, 3):
+                        weigh_gate(weighed.pop(0), nc.vector)
+                if g > 2:
+                    w_grouped.append(regroup_weights(early, len(w_grouped), nc.scalar.copy))
             w_grouped.append(regroup_weights(early, len(w_grouped), nc.scalar.copy))
+            while len(w_grouped) < 2:
+                w_grouped.append(regroup_weights(early, len(w_grouped), nc.scalar.copy))
             quantise_tokens(PASSES - 2, grouped[PASSES - 2])
             grouped.append(regroup_tokens(planes[PASSES - 1]))
-            quantise_weights(w_grouped[0])
+            quantise_weights()
             quantise_tokens(PASSES - 1, grouped[PASSES - 1])
-            quantise_weights(w_grouped[1])
+            quantise_weights()
             while len(w_grouped) < EARLY_UNITS:
                 w_grouped.append(regroup_weights(early, len(w_grouped), nc.scalar.copy))
-                quantise_weights(w_grouped[-2])
+                quantise_weights()
                 if len(gates) < STEPS:
                     make_gate(early)
-                weigh_gate(weighed.pop(0), nc.gpsimd)
-            quantise_weights(w_grouped[-1])
+            while len(quantised) < EARLY_UNITS:
+                quantise_weights()
 
         with tc.psum_pool(name="work", bufs=3, reuse_waits="tile") as work, tc.psum_pool(
             name="sums", bufs=4, reuse_waits="tile"
         ) as sums:
-            waiting = []
+            sums_of = inverse = None
+            held = []
             for step in range(STEPS):
                 n, b = divmod(step, SEQS)
                 k_ps = multiply(sums, n, b)
                 unit = EARLY_UNITS + step
                 if unit < UNITS:
                     w_grouped.append(regroup_weights(work, unit, nc.scalar.copy))
-                done = waiting[:2] if len(gates) == STEPS else []
-                waiting = waiting[len(done) :]
                 for i in range(2):
                     if len(gates) < STEPS:
                         make_gate(work, 1)
+                if inverse is not None:
+                    store_kk(*inverse, nc.gpsimd)
+                    inverse = None
                 scaled = scale_by_k_k(n, k_ps)
-                floored = [floor_sums(entry[3]) for entry in done]
+                if sums_of is not None:
+                    floored = floor_sums(sums_of[3])
                 store_k_out(n, b, k_ps, gates[step])
-                sums_of = sum_squares_on_scalar(step, scaled)
-                for entry, sum_sq in zip(done, floored):
-                    store_kk(*entry[0:3], sum_sq, nc.gpsimd)
-                if step % 2 == 0:
-                    weigh_gate(step + 1, nc.vector)
+                if weighed:
+                    weigh_gate(weighed.pop(0), nc.vector)
                 if unit < UNITS:
-                    quantise_weights(w_grouped[unit])
-                waiting.append((n, b, scaled, sums_of))
-            for entry in waiting:
-                store_kk(*entry[0:3], floor_sums(entry[3]), nc.vector)
+                    quantise_weights()
+                if sums_of is not None:
+                    inverse = sums_of[0:3] + (invert_sums(floored),)
+                    sums_of = None
+                sums_of = (n, b, scaled, sum_squares_on_scalar(step, scaled))
+            store_kk(*inverse, nc.gpsimd)
+            floored = floor_sums(sums_of[3])
+            store_kk(*(sums_of[0:3] + (invert_sums(floored),)), nc.vector)

@@ -96,12 +96,10 @@ def tile_full_tmix_params_pa_kernel(tc, x, x_k, W_k, a_hid, a2, a0, k_k, k_a, ou
         for shifted in shifted_ring:
             nc.vector.memset(shifted[:, :, 0:1], 0.0)
 
-        def transpose_tokens(banks, g, u):
-            x_t = banks.tile([P, TOKENS], F32, tag="x")
+        def transpose_tokens(banks, g, t):
+            x_t = banks.tile([P, TOKENS], BF16, tag="x", bufs=3)
             for b in range(SEQS):
-                nc.tensor.transpose(
-                    x_t[:, b * T : (b + 1) * T], x_tiles[g][:, b, :].bitcast(F32)[:, u:WORDS:2], ident_f32[:]
-                )
+                nc.tensor.transpose(x_t[:, b * T : (b + 1) * T], x_tiles[g][:, b, t:K_PASS:PACK], ident_bf[:])
             return x_t
 
         zeros = keep.tile([P, HEADS, 2], F32)
@@ -111,19 +109,17 @@ def tile_full_tmix_params_pa_kernel(tc, x, x_k, W_k, a_hid, a2, a0, k_k, k_a, ou
             nc.vector.tensor_scalar_add(out=sums_of[:], in0=zeros[:], scalar1=NORM_FLOOR * NORM_FLOOR)
 
         def mix_channels(x_t, g, t, planes):
-            e = t % 2
-            pairs = x_t[:].bitcast(BF16)
             shifted = shifted_ring[len(mixes) % len(shifted_ring)]
             mixes.append((g, t))
             nc.scalar.activation(
                 out=shifted[:, :, 1:T],
-                in_=pairs.rearrange("p (b r e) -> p b r e", b=SEQS, e=2)[:, :, 0 : T - 1, e],
+                in_=x_t[:].rearrange("p (b r) -> p b r", b=SEQS)[:, :, 0 : T - 1],
                 func=ACT.Copy,
                 scale=mix[:, t, g : g + 1],
             )
             nc.vector.scalar_tensor_tensor(
                 out=planes[:, t, :],
-                in0=pairs[:, e : 2 * TOKENS : 2],
+                in0=x_t[:],
                 scalar=stay[:, t, g : g + 1],
                 in1=shifted[:].rearrange("p b r -> p (b r)"),
                 op0=ALU.mult,
@@ -218,10 +214,10 @@ def tile_full_tmix_params_pa_kernel(tc, x, x_k, W_k, a_hid, a2, a0, k_k, k_a, ou
             )
             return scaled
 
-        def sum_squares_on_scalar(step, scaled):
+        def sum_squares_on_scalar(step, scaled, heads):
             sums_of = sum_ring[step % len(sum_ring)]
             squares = tail.tile([P, N_TILE], F32, bufs=3)
-            for h in range(HEADS):
+            for h in range(heads):
                 nc.scalar.activation(
                     out=squares[:, h * HEAD : (h + 1) * HEAD],
                     in_=scaled[:, h * HEAD : (h + 1) * HEAD],
@@ -229,6 +225,20 @@ def tile_full_tmix_params_pa_kernel(tc, x, x_k, W_k, a_hid, a2, a0, k_k, k_a, ou
                     accum_out=sums_of[:, h, 0:1],
                 )
             return sums_of
+
+        def square_on_vector(scaled, head):
+            squares = tail.tile([P, N_TILE], F32, bufs=3)
+            columns = slice(head * HEAD, N_TILE)
+            nc.vector.tensor_tensor(out=squares[:, columns], in0=scaled[:, columns], in1=scaled[:, columns], op=ALU.mult)
+            return squares
+
+        def sum_squares_on_vector(sums_of, squares, head):
+            nc.vector.tensor_reduce(
+                out=sums_of[:, head:HEADS, 0],
+                in_=squares[:, head * HEAD : N_TILE].rearrange("p (h d) -> p h d", d=HEAD),
+                axis=mybir.AxisListType.X,
+                op=ALU.add,
+            )
 
         def store_k_out(n, b, k_ps, gate):
             k_out = tail.tile([P, N_TILE], F32, bufs=5)
@@ -265,7 +275,7 @@ def tile_full_tmix_params_pa_kernel(tc, x, x_k, W_k, a_hid, a2, a0, k_k, k_a, ou
         mixes = []
 
         with tc.psum_pool(name="early", bufs=3) as early:
-            mix_ps = early.tile([P, PACK, P], BF16, tag="x")
+            mix_ps = early.tile([P, PACK, P], BF16, tag="x", bufs=3)
             for t in range(PACK):
                 nc.tensor.transpose(mix_ps[:, t, :], mix_rows[:, t:K_PASS:PACK], ident_bf[:])
             nc.vector.tensor_copy(out=mix[:], in_=mix_ps[:, :, 0:PASSES])
@@ -287,10 +297,9 @@ def tile_full_tmix_params_pa_kernel(tc, x, x_k, W_k, a_hid, a2, a0, k_k, k_a, ou
             planes, grouped = [], []
             weighed = list(range(STEPS))
             for g in range(PASSES):
-                halves = [transpose_tokens(early, g, u) for u in range(2)]
                 planes.append(stage.tile([P, PACK, TOKENS], BF16, name="planes"))
-                for i, t in enumerate((0, 2, 1, 3)):
-                    mix_channels(halves[t // 2], g, t, planes[g])
+                for i in range(PACK):
+                    mix_channels(transpose_tokens(early, g, i), g, i, planes[g])
                     if i == 0 and g > 0:
                         grouped.append(regroup_tokens(planes[g - 1]))
                     if i == 0 and g > 1:
@@ -311,8 +320,6 @@ def tile_full_tmix_params_pa_kernel(tc, x, x_k, W_k, a_hid, a2, a0, k_k, k_a, ou
                 if g > 2:
                     w_grouped.append(regroup_weights(early, len(w_grouped), nc.scalar.copy))
             w_grouped.append(regroup_weights(early, len(w_grouped), nc.scalar.copy))
-            while len(w_grouped) < 2:
-                w_grouped.append(regroup_weights(early, len(w_grouped), nc.scalar.copy))
             quantise_tokens(PASSES - 2, grouped[PASSES - 2])
             grouped.append(regroup_tokens(planes[PASSES - 1]))
             quantise_weights()
@@ -344,17 +351,24 @@ def tile_full_tmix_params_pa_kernel(tc, x, x_k, W_k, a_hid, a2, a0, k_k, k_a, ou
                     store_kk(*inverse, nc.gpsimd)
                     inverse = None
                 scaled = scale_by_k_k(n, k_ps)
+                last = step == STEPS - 1
                 if sums_of is not None:
                     floored = floor_sums(sums_of[3])
-                store_k_out(n, b, k_ps, gates[step])
-                if weighed:
-                    weigh_gate(weighed.pop(0), nc.vector)
-                if unit < UNITS:
-                    quantise_weights()
-                if sums_of is not None:
-                    inverse = sums_of[0:3] + (invert_sums(floored),)
-                    sums_of = None
-                sums_of = (n, b, scaled, sum_squares_on_scalar(step, scaled))
-            store_kk(*inverse, nc.gpsimd)
-            floored = floor_sums(sums_of[3])
-            store_kk(*(sums_of[0:3] + (invert_sums(floored),)), nc.vector)
+                if not last:
+                    store_k_out(n, b, k_ps, gates[step])
+                    if weighed:
+                        weigh_gate(weighed.pop(0), nc.vector)
+                    if unit < UNITS:
+                        quantise_weights()
+                    if sums_of is not None:
+                        inverse = sums_of[0:3] + (invert_sums(floored),)
+                    sums_of = (n, b, scaled, sum_squares_on_scalar(step, scaled, HEADS))
+            half = HEADS // 2
+            last_sums = sum_squares_on_scalar(step, scaled, half)
+            squares = square_on_vector(scaled, half)
+            inverse = sums_of[0:3] + (invert_sums(floored),)
+            sum_squares_on_vector(last_sums, squares, half)
+            store_k_out(n, b, k_ps, gates[step])
+            last_inverse = invert_sums(floor_sums(last_sums))
+            store_kk(*inverse, nc.vector)
+            store_kk(n, b, scaled, last_inverse, nc.vector)

@@ -74,10 +74,11 @@ def tile_full_tmix_params_pa_kernel(tc, x, x_k, W_k, a_hid, a2, a0, k_k, k_a, ou
             x_g = x_pool.tile([P, SEQS, K_PASS], BF16, name="x_g")
             nc.sync.dma_start(out=x_g[:], in_=x[:, :, g * K_PASS : (g + 1) * K_PASS].rearrange("b t c -> t b c"))
             x_tiles.append(x_g)
+            if g == 2:
+                nc.sync.dma_start(out=neg_k_a[:], in_=k_a.rearrange("a b c -> (a b c)").partition_broadcast(P))
             if g == 0:
                 nc.sync.dma_start(out=hid[:], in_=a_hid.rearrange("b t d -> t b d"))
                 nc.sync.dma_start(out=a2_sb[:], in_=a2)
-        nc.sync.dma_start(out=neg_k_a[:], in_=k_a.rearrange("a b c -> (a b c)").partition_broadcast(P))
         w_tiles = []
         for i in range(CO // P):
             w_i = w_pool.tile([P, C], BF16, name="w_i")
@@ -226,10 +227,10 @@ def tile_full_tmix_params_pa_kernel(tc, x, x_k, W_k, a_hid, a2, a0, k_k, k_a, ou
                 )
             return sums_of
 
-        def square_on_vector(scaled, head):
+        def square(scaled, head):
             squares = tail.tile([P, N_TILE], F32, bufs=3)
             columns = slice(head * HEAD, N_TILE)
-            nc.vector.tensor_tensor(out=squares[:, columns], in0=scaled[:, columns], in1=scaled[:, columns], op=ALU.mult)
+            nc.scalar.activation(out=squares[:, columns], in_=scaled[:, columns], func=ACT.Square)
             return squares
 
         def sum_squares_on_vector(sums_of, squares, head):
@@ -286,14 +287,16 @@ def tile_full_tmix_params_pa_kernel(tc, x, x_k, W_k, a_hid, a2, a0, k_k, k_a, ou
             nc.tensor.transpose(a0_ps[:], a0_rows[:], ident_bf[:])
             a0_one = keep.tile([P, CO // P], F32)
             nc.scalar.copy(out=a0_one[:], in_=a0_ps[:, 0 : CO // P])
-            nc.gpsimd.tensor_scalar(
-                out=a0_cols[:],
-                in0=a0_one[:].unsqueeze(2).to_broadcast([P, CO // P, P]),
-                scalar1=1.0,
-                scalar2=0.0,
-                op0=ALU.mult,
-                op1=ALU.add,
-            )
+            for n in range(N_TILES):
+                blocks = slice(n * BLOCKS, (n + 1) * BLOCKS)
+                nc.gpsimd.tensor_scalar(
+                    out=a0_cols[:, blocks, :],
+                    in0=a0_one[:, blocks].unsqueeze(2).to_broadcast([P, BLOCKS, P]),
+                    scalar1=1.0,
+                    scalar2=0.0,
+                    op0=ALU.mult,
+                    op1=ALU.add,
+                )
             planes, grouped = [], []
             weighed = list(range(STEPS))
             for g in range(PASSES):
@@ -302,14 +305,14 @@ def tile_full_tmix_params_pa_kernel(tc, x, x_k, W_k, a_hid, a2, a0, k_k, k_a, ou
                     mix_channels(transpose_tokens(early, g, i), g, i, planes[g])
                     if i == 0 and g > 0:
                         grouped.append(regroup_tokens(planes[g - 1]))
-                    if i == 0 and g > 1:
+                    if i == 2 and g > 1:
                         quantise_tokens(g - 2, grouped[g - 2])
                     if g == 0 and i == 0:
                         hid_ps = early.tile([P, TOKENS], BF16, tag="z", bufs=2)
                         for b in range(SEQS):
                             nc.tensor.transpose(hid_ps[:, b * T : (b + 1) * T], hid[:, b, :], ident_bf[:])
                         nc.scalar.copy(out=hid_t[:], in_=hid_ps[:])
-                    if g > 0 or i > 0:
+                    if g > 0 or i > 1:
                         make_gate(early)
                     if g == 1 and i == 0:
                         nc.vector.tensor_scalar(
@@ -332,6 +335,7 @@ def tile_full_tmix_params_pa_kernel(tc, x, x_k, W_k, a_hid, a2, a0, k_k, k_a, ou
                     make_gate(early)
             while len(quantised) < EARLY_UNITS:
                 quantise_weights()
+            nc.scalar.sqrt(out=warm[:, 1:2], in_=warm[:, 0:1])
 
         with tc.psum_pool(name="work", bufs=3, reuse_waits="tile") as work, tc.psum_pool(
             name="sums", bufs=4, reuse_waits="tile"
@@ -344,9 +348,6 @@ def tile_full_tmix_params_pa_kernel(tc, x, x_k, W_k, a_hid, a2, a0, k_k, k_a, ou
                 unit = EARLY_UNITS + step
                 if unit < UNITS:
                     w_grouped.append(regroup_weights(work, unit, nc.scalar.copy))
-                for i in range(2):
-                    if len(gates) < STEPS:
-                        make_gate(work, 1)
                 if inverse is not None:
                     store_kk(*inverse, nc.gpsimd)
                     inverse = None
@@ -364,8 +365,8 @@ def tile_full_tmix_params_pa_kernel(tc, x, x_k, W_k, a_hid, a2, a0, k_k, k_a, ou
                         inverse = sums_of[0:3] + (invert_sums(floored),)
                     sums_of = (n, b, scaled, sum_squares_on_scalar(step, scaled, HEADS))
             half = HEADS // 2
+            squares = square(scaled, half)
             last_sums = sum_squares_on_scalar(step, scaled, half)
-            squares = square_on_vector(scaled, half)
             inverse = sums_of[0:3] + (invert_sums(floored),)
             sum_squares_on_vector(last_sums, squares, half)
             store_k_out(n, b, k_ps, gates[step])

@@ -253,14 +253,17 @@ def tile_full_tmix_params_pa_kernel(tc, x, x_k, W_k, a_hid, a2, a0, k_k, k_a, ou
             nc.vector.tensor_reduce(out=floored[:], in_=sums_of[:], axis=mybir.AxisListType.X, op=ALU.max)
             return floored
 
-        def invert_sums(floored):
-            inv_sq = tail.tile([P, HEADS], F32)
-            nc.vector.reciprocal(out=inv_sq[:], in_=floored[:])
-            return inv_sq
+        def root_sums(floored):
+            norm = tail.tile([P, HEADS], F32, bufs=4)
+            nc.scalar.sqrt(out=norm[:], in_=floored[:])
+            return norm
 
-        def store_kk(n, b, scaled, inv_sq, multiplier):
+        def invert(norm):
             inv_norm = tail.tile([P, HEADS], F32)
-            nc.scalar.sqrt(out=inv_norm[:], in_=inv_sq[:])
+            nc.vector.reciprocal(out=inv_norm[:], in_=norm[:])
+            return inv_norm
+
+        def store_kk(n, b, scaled, inv_norm, multiplier):
             kk = tail.tile([P, N_TILE], F32, bufs=5)
             multiplier.tensor_tensor(
                 out=kk[:].rearrange("p (h d) -> p h d", d=HEAD),
@@ -340,36 +343,32 @@ def tile_full_tmix_params_pa_kernel(tc, x, x_k, W_k, a_hid, a2, a0, k_k, k_a, ou
         with tc.psum_pool(name="work", bufs=3, reuse_waits="tile") as work, tc.psum_pool(
             name="sums", bufs=4, reuse_waits="tile"
         ) as sums:
-            sums_of = inverse = None
-            held = []
+            summed = rooted = None
             for step in range(STEPS):
                 n, b = divmod(step, SEQS)
-                k_ps = multiply(sums, n, b)
-                unit = EARLY_UNITS + step
-                if unit < UNITS:
-                    w_grouped.append(regroup_weights(work, unit, nc.scalar.copy))
-                if inverse is not None:
-                    store_kk(*inverse, nc.gpsimd)
-                    inverse = None
-                scaled = scale_by_k_k(n, k_ps)
                 last = step == STEPS - 1
-                if sums_of is not None:
-                    floored = floor_sums(sums_of[3])
+                k_ps = multiply(sums, n, b)
+                if len(w_grouped) < UNITS:
+                    w_grouped.append(regroup_weights(work, len(w_grouped), nc.scalar.copy))
+                scaled = scale_by_k_k(n, k_ps)
+                half = HEADS // 2 if last else HEADS
+                if last:
+                    squares = square(scaled, half)
+                sums_of = sum_squares_on_scalar(step, scaled, half)
+                if summed is not None:
+                    norm = root_sums(floor_sums(summed[3]))
                 if not last:
                     store_k_out(n, b, k_ps, gates[step])
                     if weighed:
                         weigh_gate(weighed.pop(0), nc.vector)
-                    if unit < UNITS:
-                        quantise_weights()
-                    if sums_of is not None:
-                        inverse = sums_of[0:3] + (invert_sums(floored),)
-                    sums_of = (n, b, scaled, sum_squares_on_scalar(step, scaled, HEADS))
-            half = HEADS // 2
-            squares = square(scaled, half)
-            last_sums = sum_squares_on_scalar(step, scaled, half)
-            inverse = sums_of[0:3] + (invert_sums(floored),)
-            sum_squares_on_vector(last_sums, squares, half)
+                if rooted is not None:
+                    store_kk(*rooted[0:3], invert(rooted[3]), nc.gpsimd)
+                if len(quantised) < UNITS:
+                    quantise_weights()
+                rooted = summed[0:3] + (norm,) if summed is not None else None
+                summed = (n, b, scaled, sums_of)
+            sum_squares_on_vector(sums_of, squares, half)
             store_k_out(n, b, k_ps, gates[step])
-            last_inverse = invert_sums(floor_sums(last_sums))
-            store_kk(*inverse, nc.vector)
-            store_kk(n, b, scaled, last_inverse, nc.vector)
+            last_norm = root_sums(floor_sums(sums_of))
+            store_kk(*rooted[0:3], invert(rooted[3]), nc.vector)
+            store_kk(n, b, scaled, invert(last_norm), nc.vector)

@@ -355,14 +355,15 @@ def tile_full_tmix_params_pa_kernel(tc, x, x_k, W_k, a_hid, a2, a0, k_k, k_a, ou
                 if last:
                     squares = square(scaled, half)
                 sums_of = sum_squares_on_scalar(step, scaled, half)
-                if summed is not None:
-                    norm = root_sums(floor_sums(summed[3]))
                 if not last:
                     store_k_out(n, b, k_ps, gates[step])
-                    if weighed:
-                        weigh_gate(weighed.pop(0), nc.vector)
+                if summed is not None:
+                    norm = root_sums(floor_sums(summed[3]))
                 if rooted is not None:
                     store_kk(*rooted[0:3], invert(rooted[3]), nc.gpsimd)
+                if not last:
+                    if weighed:
+                        weigh_gate(weighed.pop(0), nc.vector)
                 if len(quantised) < UNITS:
                     quantise_weights()
                 rooted = summed[0:3] + (norm,) if summed is not None else None

@@ -33,6 +33,7 @@ UNITS = N_TILES * PASSES
 EARLY_UNITS = 5
 STEPS = N_TILES * SEQS
 NORM_FLOOR = 1e-12
+TINY = 1e-30
 
 FLOPS = 2 * TOKENS * C * CO + 2 * TOKENS * DA * CO
 
@@ -50,7 +51,7 @@ def tile_full_tmix_params_pa_kernel(tc, x, x_k, W_k, a_hid, a2, a0, k_k, k_a, ou
         tail = ctx.enter_context(tc.tile_pool(name="tail", bufs=3))
 
         warm = keep.tile([P, 2], F32)
-        nc.vector.memset(warm[:], 0.0)
+        nc.vector.memset(warm[:], 1.0)
         nc.scalar.activation(out=warm[:, 1:2], in_=warm[:, 0:1], func=ACT.Sigmoid)
 
         ident_bf = keep.tile([P, P], BF16)
@@ -65,17 +66,24 @@ def tile_full_tmix_params_pa_kernel(tc, x, x_k, W_k, a_hid, a2, a0, k_k, k_a, ou
         hid = keep.tile([P, SEQS, DA], BF16)
         a2_sb = keep.tile([DA, CO], BF16)
         k_k_all = keep.tile([P, CO], BF16)
-        neg_k_a = keep.tile([P, CO], BF16)
+        k_a_all = keep.tile([P, CO], BF16)
 
-        nc.sync.dma_start(out=mix_rows[0:PASSES, :], in_=x_k.rearrange("a b (r c) -> (a b r) c", c=K_PASS))
-        nc.sync.dma_start(out=a0_rows[0 : CO // P, :], in_=a0.rearrange("a b (j p) -> (a b j) p", p=P))
+        nc.scalar.dma_start(out=mix_rows[0:PASSES, :], in_=x_k.rearrange("a b (r c) -> (a b r) c", c=K_PASS))
+        nc.scalar.dma_start(out=a0_rows[0 : CO // P, :], in_=a0.rearrange("a b (j p) -> (a b j) p", p=P))
+
+        def load_on_all(tile, vector, n):
+            columns = slice(n * N_TILE, (n + 1) * N_TILE)
+            nc.sync.dma_start(
+                out=tile[:, columns], in_=vector.rearrange("a b c -> (a b c)")[columns].partition_broadcast(P)
+            )
+
         x_tiles = []
         for g in range(PASSES):
             x_g = x_pool.tile([P, SEQS, K_PASS], BF16, name="x_g")
             nc.sync.dma_start(out=x_g[:], in_=x[:, :, g * K_PASS : (g + 1) * K_PASS].rearrange("b t c -> t b c"))
             x_tiles.append(x_g)
-            if g == 2:
-                nc.sync.dma_start(out=neg_k_a[:], in_=k_a.rearrange("a b c -> (a b c)").partition_broadcast(P))
+            if g > 1:
+                load_on_all(k_a_all, k_a, g - 2)
             if g == 0:
                 nc.sync.dma_start(out=hid[:], in_=a_hid.rearrange("b t d -> t b d"))
                 nc.sync.dma_start(out=a2_sb[:], in_=a2)
@@ -84,8 +92,10 @@ def tile_full_tmix_params_pa_kernel(tc, x, x_k, W_k, a_hid, a2, a0, k_k, k_a, ou
             w_i = w_pool.tile([P, C], BF16, name="w_i")
             nc.sync.dma_start(out=w_i[:], in_=W_k[i * P : (i + 1) * P, :])
             w_tiles.append(w_i)
-            if i == BLOCKS - 1:
-                nc.sync.dma_start(out=k_k_all[:], in_=k_k.rearrange("a b c -> (a b c)").partition_broadcast(P))
+            if i % BLOCKS == BLOCKS - 1:
+                load_on_all(k_k_all, k_k, i // BLOCKS)
+                if i // BLOCKS + 2 < N_TILES:
+                    load_on_all(k_a_all, k_a, i // BLOCKS + 2)
 
         mix = keep.tile([P, PACK, PASSES], F32)
         stay = keep.tile([P, PACK, PASSES], F32)
@@ -105,9 +115,11 @@ def tile_full_tmix_params_pa_kernel(tc, x, x_k, W_k, a_hid, a2, a0, k_k, k_a, ou
 
         zeros = keep.tile([P, HEADS, 2], F32)
         nc.vector.memset(zeros[:], 0.0)
-        sum_ring = [keep.tile([P, HEADS, 2], F32, name="sums%d" % i) for i in range(4)]
-        for sums_of in sum_ring:
-            nc.vector.tensor_scalar_add(out=sums_of[:], in0=zeros[:], scalar1=NORM_FLOOR * NORM_FLOOR)
+        inverse_ring = [keep.tile([P, HEADS, 2], F32, name="inverses%d" % i) for i in range(4)]
+        for inverses in inverse_ring:
+            nc.vector.tensor_scalar_add(out=inverses[:], in0=zeros[:], scalar1=1.0 / NORM_FLOOR)
+        tiny = keep.tile([P, 1], F32)
+        nc.vector.tensor_scalar_add(out=tiny[:], in0=zeros[:, 0, 0:1], scalar1=TINY)
 
         def mix_channels(x_t, g, t, planes):
             shifted = shifted_ring[len(mixes) % len(shifted_ring)]
@@ -187,10 +199,15 @@ def tile_full_tmix_params_pa_kernel(tc, x, x_k, W_k, a_hid, a2, a0, k_k, k_a, ou
             nc.scalar.activation(out=gate[:], in_=z_ps[:], func=ACT.Sigmoid, scale=-1.0)
             gates.append(gate)
 
-        def weigh_gate(step, multiplier):
+        def weigh_gate(step):
             n = step // SEQS
-            multiplier.tensor_tensor(
-                out=gates[step][:], in0=gates[step][:], in1=neg_k_a[:, n * N_TILE : (n + 1) * N_TILE], op=ALU.mult
+            nc.vector.scalar_tensor_tensor(
+                out=gates[step][:],
+                in0=gates[step][:],
+                scalar=-1.0,
+                in1=k_a_all[:, n * N_TILE : (n + 1) * N_TILE],
+                op0=ALU.mult,
+                op1=ALU.mult,
             )
 
         def multiply(sums, n, b):
@@ -216,14 +233,14 @@ def tile_full_tmix_params_pa_kernel(tc, x, x_k, W_k, a_hid, a2, a0, k_k, k_a, ou
             return scaled
 
         def sum_squares_on_scalar(step, scaled, heads):
-            sums_of = sum_ring[step % len(sum_ring)]
+            sums_of = tail.tile([P, HEADS], F32, name="sums_of", bufs=3)
             squares = tail.tile([P, N_TILE], F32, bufs=3)
             for h in range(heads):
                 nc.scalar.activation(
                     out=squares[:, h * HEAD : (h + 1) * HEAD],
                     in_=scaled[:, h * HEAD : (h + 1) * HEAD],
                     func=ACT.Square,
-                    accum_out=sums_of[:, h, 0:1],
+                    accum_out=sums_of[:, h : h + 1],
                 )
             return sums_of
 
@@ -235,7 +252,7 @@ def tile_full_tmix_params_pa_kernel(tc, x, x_k, W_k, a_hid, a2, a0, k_k, k_a, ou
 
         def sum_squares_on_vector(sums_of, squares, head):
             nc.vector.tensor_reduce(
-                out=sums_of[:, head:HEADS, 0],
+                out=sums_of[:, head:HEADS],
                 in_=squares[:, head * HEAD : N_TILE].rearrange("p (h d) -> p h d", d=HEAD),
                 axis=mybir.AxisListType.X,
                 op=ALU.add,
@@ -248,19 +265,16 @@ def tile_full_tmix_params_pa_kernel(tc, x, x_k, W_k, a_hid, a2, a0, k_k, k_a, ou
             )
             nc.sync.dma_start(out=out_0[b, :, n * N_TILE : (n + 1) * N_TILE], in_=k_out[:])
 
-        def floor_sums(sums_of):
-            floored = tail.tile([P, HEADS], F32)
-            nc.vector.tensor_reduce(out=floored[:], in_=sums_of[:], axis=mybir.AxisListType.X, op=ALU.max)
-            return floored
+        def invert_norm(step, sums_of):
+            inverses = inverse_ring[step % len(inverse_ring)]
+            nc.scalar.activation(
+                out=inverses[:, :, 0], in_=sums_of[:], func=ACT.Abs_reciprocal_sqrt, bias=tiny[:]
+            )
+            return inverses
 
-        def root_sums(floored):
-            norm = tail.tile([P, HEADS], F32, bufs=4)
-            nc.scalar.sqrt(out=norm[:], in_=floored[:])
-            return norm
-
-        def invert(norm):
+        def cap(inverses):
             inv_norm = tail.tile([P, HEADS], F32)
-            nc.vector.reciprocal(out=inv_norm[:], in_=norm[:])
+            nc.vector.tensor_reduce(out=inv_norm[:], in_=inverses[:], axis=mybir.AxisListType.X, op=ALU.min)
             return inv_norm
 
         def store_kk(n, b, scaled, inv_norm, multiplier):
@@ -317,12 +331,8 @@ def tile_full_tmix_params_pa_kernel(tc, x, x_k, W_k, a_hid, a2, a0, k_k, k_a, ou
                         nc.scalar.copy(out=hid_t[:], in_=hid_ps[:])
                     if g > 0 or i > 1:
                         make_gate(early)
-                    if g == 1 and i == 0:
-                        nc.vector.tensor_scalar(
-                            out=neg_k_a[:], in0=neg_k_a[:], scalar1=-1.0, scalar2=None, op0=ALU.mult
-                        )
-                    if g > 0 and i in (2, 3):
-                        weigh_gate(weighed.pop(0), nc.vector)
+                    if g > 1 and i > 0:
+                        weigh_gate(weighed.pop(0))
                 if g > 2:
                     w_grouped.append(regroup_weights(early, len(w_grouped), nc.scalar.copy))
             w_grouped.append(regroup_weights(early, len(w_grouped), nc.scalar.copy))
@@ -338,18 +348,20 @@ def tile_full_tmix_params_pa_kernel(tc, x, x_k, W_k, a_hid, a2, a0, k_k, k_a, ou
                     make_gate(early)
             while len(quantised) < EARLY_UNITS:
                 quantise_weights()
-            nc.scalar.sqrt(out=warm[:, 1:2], in_=warm[:, 0:1])
+            nc.scalar.activation(out=warm[:, 1:2], in_=warm[:, 0:1], func=ACT.Abs_reciprocal_sqrt)
 
         with tc.psum_pool(name="work", bufs=3, reuse_waits="tile") as work, tc.psum_pool(
             name="sums", bufs=4, reuse_waits="tile"
         ) as sums:
-            summed = rooted = None
+            summed = None
             for step in range(STEPS):
                 n, b = divmod(step, SEQS)
                 last = step == STEPS - 1
                 k_ps = multiply(sums, n, b)
                 if len(w_grouped) < UNITS:
                     w_grouped.append(regroup_weights(work, len(w_grouped), nc.scalar.copy))
+                if summed is not None:
+                    inverses = invert_norm(step - 1, summed[3])
                 scaled = scale_by_k_k(n, k_ps)
                 half = HEADS // 2 if last else HEADS
                 if last:
@@ -357,19 +369,17 @@ def tile_full_tmix_params_pa_kernel(tc, x, x_k, W_k, a_hid, a2, a0, k_k, k_a, ou
                 sums_of = sum_squares_on_scalar(step, scaled, half)
                 if not last:
                     store_k_out(n, b, k_ps, gates[step])
-                if summed is not None:
-                    norm = root_sums(floor_sums(summed[3]))
-                if rooted is not None:
-                    store_kk(*rooted[0:3], invert(rooted[3]), nc.gpsimd)
+                if summed is not None and not last:
+                    store_kk(*summed[0:3], cap(inverses), nc.gpsimd)
                 if not last:
                     if weighed:
-                        weigh_gate(weighed.pop(0), nc.vector)
+                        weigh_gate(weighed.pop(0))
                 if len(quantised) < UNITS:
                     quantise_weights()
-                rooted = summed[0:3] + (norm,) if summed is not None else None
+                before = summed
                 summed = (n, b, scaled, sums_of)
             sum_squares_on_vector(sums_of, squares, half)
             store_k_out(n, b, k_ps, gates[step])
-            last_norm = root_sums(floor_sums(sums_of))
-            store_kk(*rooted[0:3], invert(rooted[3]), nc.vector)
-            store_kk(n, b, scaled, invert(last_norm), nc.vector)
+            last_inverses = invert_norm(step, sums_of)
+            store_kk(*before[0:3], cap(inverses), nc.vector)
+            store_kk(n, b, scaled, cap(last_inverses), nc.vector)

@@ -68,14 +68,18 @@ def tile_full_tmix_params_pa_kernel(tc, x, x_k, W_k, a_hid, a2, a0, k_k, k_a, ou
         k_k_all = keep.tile([P, CO], BF16)
         k_a_all = keep.tile([P, CO], BF16)
 
-        nc.scalar.dma_start(out=mix_rows[0:PASSES, :], in_=x_k.rearrange("a b (r c) -> (a b r) c", c=K_PASS))
-        nc.scalar.dma_start(out=a0_rows[0 : CO // P, :], in_=a0.rearrange("a b (j p) -> (a b j) p", p=P))
+        nc.sync.dma_start(out=mix_rows[0:PASSES, :], in_=x_k.rearrange("a b (r c) -> (a b r) c", c=K_PASS))
+        nc.sync.dma_start(out=a0_rows[0 : CO // P, :], in_=a0.rearrange("a b (j p) -> (a b j) p", p=P))
 
         def load_on_all(tile, vector, n):
             columns = slice(n * N_TILE, (n + 1) * N_TILE)
             nc.sync.dma_start(
                 out=tile[:, columns], in_=vector.rearrange("a b c -> (a b c)")[columns].partition_broadcast(P)
             )
+
+        def load_a2(n):
+            columns = slice(n * N_TILE, (n + 1) * N_TILE)
+            nc.sync.dma_start(out=a2_sb[:, columns], in_=a2[:, columns])
 
         x_tiles = []
         for g in range(PASSES):
@@ -86,7 +90,9 @@ def tile_full_tmix_params_pa_kernel(tc, x, x_k, W_k, a_hid, a2, a0, k_k, k_a, ou
                 load_on_all(k_a_all, k_a, g - 2)
             if g == 0:
                 nc.sync.dma_start(out=hid[:], in_=a_hid.rearrange("b t d -> t b d"))
-                nc.sync.dma_start(out=a2_sb[:], in_=a2)
+                load_a2(0)
+            else:
+                load_a2(g)
         w_tiles = []
         for i in range(CO // P):
             w_i = w_pool.tile([P, C], BF16, name="w_i")
@@ -99,7 +105,6 @@ def tile_full_tmix_params_pa_kernel(tc, x, x_k, W_k, a_hid, a2, a0, k_k, k_a, ou
 
         mix = keep.tile([P, PACK, PASSES], F32)
         stay = keep.tile([P, PACK, PASSES], F32)
-        a0_cols = keep.tile([P, CO // P, P], F32)
         hid_t = keep.tile([DA, TOKENS], BF16)
         xk_codes = keep.tile([P, PASSES, TOKENS], U32, align_bytes=64)
         xk_scales = keep.tile([P, PASSES, TOKENS], U8, align_bytes=64)
@@ -189,7 +194,7 @@ def tile_full_tmix_params_pa_kernel(tc, x, x_k, W_k, a_hid, a2, a0, k_k, k_a, ou
                 j = n * BLOCKS + i
                 nc.tensor.matmul(
                     z_ps[:, i * P : (i + 1) * P],
-                    lhsT=a0_cols[:, j, :],
+                    lhsT=a0_one[:, j : j + 1].to_broadcast([P, P]),
                     rhs=ident_f32[:],
                     is_transpose=True,
                     start=False,
@@ -287,6 +292,18 @@ def tile_full_tmix_params_pa_kernel(tc, x, x_k, W_k, a_hid, a2, a0, k_k, k_a, ou
             )
             nc.sync.dma_start(out=out_1[b, :, n * N_TILE : (n + 1) * N_TILE], in_=kk[:])
 
+        def cap_and_store_kk(n, b, scaled, inverses):
+            kk = tail.tile([P, N_TILE], F32, bufs=5)
+            nc.vector.scalar_tensor_tensor(
+                out=kk[:].rearrange("p (h d) -> p h d", d=HEAD),
+                in0=inverses[:, :, 0:1].to_broadcast([P, HEADS, HEAD]),
+                scalar=1.0 / NORM_FLOOR,
+                in1=scaled[:].rearrange("p (h d) -> p h d", d=HEAD),
+                op0=ALU.min,
+                op1=ALU.mult,
+            )
+            nc.sync.dma_start(out=out_1[b, :, n * N_TILE : (n + 1) * N_TILE], in_=kk[:])
+
         w_grouped = []
         quantised = []
         gates = []
@@ -303,17 +320,7 @@ def tile_full_tmix_params_pa_kernel(tc, x, x_k, W_k, a_hid, a2, a0, k_k, k_a, ou
             a0_ps = early.tile([P, P], BF16, tag="z", bufs=2)
             nc.tensor.transpose(a0_ps[:], a0_rows[:], ident_bf[:])
             a0_one = keep.tile([P, CO // P], F32)
-            nc.scalar.copy(out=a0_one[:], in_=a0_ps[:, 0 : CO // P])
-            for n in range(N_TILES):
-                blocks = slice(n * BLOCKS, (n + 1) * BLOCKS)
-                nc.gpsimd.tensor_scalar(
-                    out=a0_cols[:, blocks, :],
-                    in0=a0_one[:, blocks].unsqueeze(2).to_broadcast([P, BLOCKS, P]),
-                    scalar1=1.0,
-                    scalar2=0.0,
-                    op0=ALU.mult,
-                    op1=ALU.add,
-                )
+            nc.vector.tensor_copy(out=a0_one[:], in_=a0_ps[:, 0 : CO // P])
             planes, grouped = [], []
             weighed = list(range(STEPS))
             for g in range(PASSES):
@@ -328,7 +335,7 @@ def tile_full_tmix_params_pa_kernel(tc, x, x_k, W_k, a_hid, a2, a0, k_k, k_a, ou
                         hid_ps = early.tile([P, TOKENS], BF16, tag="z", bufs=2)
                         for b in range(SEQS):
                             nc.tensor.transpose(hid_ps[:, b * T : (b + 1) * T], hid[:, b, :], ident_bf[:])
-                        nc.scalar.copy(out=hid_t[:], in_=hid_ps[:])
+                        nc.vector.tensor_copy(out=hid_t[:], in_=hid_ps[:])
                     if g > 0 or i > 1:
                         make_gate(early)
                     if g > 1 and i > 0:
@@ -367,8 +374,7 @@ def tile_full_tmix_params_pa_kernel(tc, x, x_k, W_k, a_hid, a2, a0, k_k, k_a, ou
                 if last:
                     squares = square(scaled, half)
                 sums_of = sum_squares_on_scalar(step, scaled, half)
-                if not last:
-                    store_k_out(n, b, k_ps, gates[step])
+                store_k_out(n, b, k_ps, gates[step])
                 if summed is not None and not last:
                     store_kk(*summed[0:3], cap(inverses), nc.gpsimd)
                 if not last:
@@ -379,7 +385,6 @@ def tile_full_tmix_params_pa_kernel(tc, x, x_k, W_k, a_hid, a2, a0, k_k, k_a, ou
                 before = summed
                 summed = (n, b, scaled, sums_of)
             sum_squares_on_vector(sums_of, squares, half)
-            store_k_out(n, b, k_ps, gates[step])
             last_inverses = invert_norm(step, sums_of)
-            store_kk(*before[0:3], cap(inverses), nc.vector)
-            store_kk(n, b, scaled, cap(last_inverses), nc.vector)
+            cap_and_store_kk(*before[0:3], inverses)
+            cap_and_store_kk(n, b, scaled, last_inverses)

@@ -1,7 +1,6 @@
 from contextlib import ExitStack
 
 import concourse.mybir as mybir
-from concourse.masks import make_identity
 
 BF16 = mybir.dt.bfloat16
 F32 = mybir.dt.float32
@@ -33,6 +32,7 @@ UNITS = N_TILES * PASSES
 EARLY_UNITS = 5
 STEPS = N_TILES * SEQS
 NORM_FLOOR = 1e-12
+SQUARE = 32
 TINY = 1e-30
 
 FLOPS = 2 * TOKENS * C * CO + 2 * TOKENS * DA * CO
@@ -54,22 +54,38 @@ def tile_full_tmix_params_pa_kernel(tc, x, x_k, W_k, a_hid, a2, a0, k_k, k_a, ou
         nc.vector.memset(warm[:], 1.0)
         nc.scalar.activation(out=warm[:, 1:2], in_=warm[:, 0:1], func=ACT.Sigmoid)
 
-        ident_bf = keep.tile([P, P], BF16)
-        make_identity(nc, ident_bf[:])
-        ident_f32 = keep.tile([P, P], F32)
-        make_identity(nc, ident_f32[:])
+        ones = keep.tile([P, P], F32)
+        nc.vector.memset(ones[:], 1.0)
 
         mix_rows = keep.tile([P, K_PASS], BF16)
         nc.vector.memset(mix_rows[:], 0.0)
         a0_rows = keep.tile([P, P], BF16)
         nc.vector.memset(a0_rows[:], 0.0)
+
+        columns_of = keep.tile([P, P], F32, align_bytes=64)
+        nc.vector.tensor_tensor_scan(
+            out=columns_of[:], data0=ones[:], data1=ones[:], initial=-1.0, op0=ALU.mult, op1=ALU.add
+        )
+        rows_of = keep.tile([P, P], F32, align_bytes=64)
+        nc.vector.transpose(out=rows_of[:], in_=columns_of[:])
+        ident_bf = keep.tile([P, P], BF16)
+        for block in range(0, P, SQUARE):
+            lines = slice(block, block + SQUARE)
+            nc.vector.tensor_scalar(
+                out=ident_bf[lines, :],
+                in0=columns_of[lines, :],
+                scalar1=rows_of[lines, 0:1],
+                scalar2=float(block),
+                op0=ALU.subtract,
+                op1=ALU.is_equal,
+            )
+        ident_f32 = keep.tile([P, P], F32)
+        nc.vector.tensor_copy(out=ident_f32[:], in_=ident_bf[:])
         hid = keep.tile([P, SEQS, DA], BF16)
         a2_sb = keep.tile([DA, CO], BF16)
         k_k_all = keep.tile([P, CO], BF16)
         k_a_all = keep.tile([P, CO], BF16)
 
-        nc.sync.dma_start(out=mix_rows[0:PASSES, :], in_=x_k.rearrange("a b (r c) -> (a b r) c", c=K_PASS))
-        nc.sync.dma_start(out=a0_rows[0 : CO // P, :], in_=a0.rearrange("a b (j p) -> (a b j) p", p=P))
 
         def load_on_all(tile, vector, n):
             columns = slice(n * N_TILE, (n + 1) * N_TILE)
@@ -77,22 +93,19 @@ def tile_full_tmix_params_pa_kernel(tc, x, x_k, W_k, a_hid, a2, a0, k_k, k_a, ou
                 out=tile[:, columns], in_=vector.rearrange("a b c -> (a b c)")[columns].partition_broadcast(P)
             )
 
-        def load_a2(n):
-            columns = slice(n * N_TILE, (n + 1) * N_TILE)
-            nc.sync.dma_start(out=a2_sb[:, columns], in_=a2[:, columns])
-
         x_tiles = []
         for g in range(PASSES):
             x_g = x_pool.tile([P, SEQS, K_PASS], BF16, name="x_g")
             nc.sync.dma_start(out=x_g[:], in_=x[:, :, g * K_PASS : (g + 1) * K_PASS].rearrange("b t c -> t b c"))
             x_tiles.append(x_g)
+            if g == 0:
+                nc.sync.dma_start(out=mix_rows[0:PASSES, :], in_=x_k.rearrange("a b (r c) -> (a b r) c", c=K_PASS))
+                nc.sync.dma_start(out=a0_rows[0 : CO // P, :], in_=a0.rearrange("a b (j p) -> (a b j) p", p=P))
             if g > 1:
                 load_on_all(k_a_all, k_a, g - 2)
             if g == 0:
                 nc.sync.dma_start(out=hid[:], in_=a_hid.rearrange("b t d -> t b d"))
-                load_a2(0)
-            else:
-                load_a2(g)
+                nc.sync.dma_start(out=a2_sb[:], in_=a2)
         w_tiles = []
         for i in range(CO // P):
             w_i = w_pool.tile([P, C], BF16, name="w_i")
@@ -336,7 +349,7 @@ def tile_full_tmix_params_pa_kernel(tc, x, x_k, W_k, a_hid, a2, a0, k_k, k_a, ou
                         for b in range(SEQS):
                             nc.tensor.transpose(hid_ps[:, b * T : (b + 1) * T], hid[:, b, :], ident_bf[:])
                         nc.vector.tensor_copy(out=hid_t[:], in_=hid_ps[:])
-                    if g > 0 or i > 1:
+                    if g > 0 or i > 2:
                         make_gate(early)
                     if g > 1 and i > 0:
                         weigh_gate(weighed.pop(0))

@@ -32,6 +32,7 @@ UNITS = N_TILES * PASSES
 EARLY_UNITS = 5
 STEPS = N_TILES * SEQS
 NORM_FLOOR = 1e-12
+SCALAR_HEADS = 2
 SQUARE = 32
 TINY = 1e-30
 
@@ -295,14 +296,21 @@ def tile_full_tmix_params_pa_kernel(tc, x, x_k, W_k, a_hid, a2, a0, k_k, k_a, ou
             nc.vector.tensor_reduce(out=inv_norm[:], in_=inverses[:], axis=mybir.AxisListType.X, op=ALU.min)
             return inv_norm
 
-        def store_kk(n, b, scaled, inv_norm, multiplier):
+        def store_kk(n, b, scaled, inv_norm):
             kk = tail.tile([P, N_TILE], F32, bufs=5)
-            multiplier.tensor_tensor(
-                out=kk[:].rearrange("p (h d) -> p h d", d=HEAD),
-                in0=scaled[:].rearrange("p (h d) -> p h d", d=HEAD),
-                in1=inv_norm[:].unsqueeze(2).to_broadcast([P, HEADS, HEAD]),
+            shared = HEADS - SCALAR_HEADS
+            columns = slice(0, shared * HEAD)
+            nc.gpsimd.tensor_tensor(
+                out=kk[:, columns].rearrange("p (h d) -> p h d", d=HEAD),
+                in0=scaled[:, columns].rearrange("p (h d) -> p h d", d=HEAD),
+                in1=inv_norm[:, 0:shared].unsqueeze(2).to_broadcast([P, shared, HEAD]),
                 op=ALU.mult,
             )
+            for h in range(shared, HEADS):
+                columns = slice(h * HEAD, (h + 1) * HEAD)
+                nc.scalar.activation(
+                    out=kk[:, columns], in_=scaled[:, columns], func=ACT.Copy, scale=inv_norm[:, h : h + 1]
+                )
             nc.sync.dma_start(out=out_1[b, :, n * N_TILE : (n + 1) * N_TILE], in_=kk[:])
 
         def cap_and_store_kk(n, b, scaled, inverses):
@@ -389,7 +397,7 @@ def tile_full_tmix_params_pa_kernel(tc, x, x_k, W_k, a_hid, a2, a0, k_k, k_a, ou
                 sums_of = sum_squares_on_scalar(step, scaled, half)
                 store_k_out(n, b, k_ps, gates[step])
                 if summed is not None and not last:
-                    store_kk(*summed[0:3], cap(inverses), nc.gpsimd)
+                    store_kk(*summed[0:3], cap(inverses))
                 if not last:
                     if weighed:
                         weigh_gate(weighed.pop(0))

@@ -32,7 +32,8 @@ UNITS = N_TILES * PASSES
 EARLY_UNITS = 5
 STEPS = N_TILES * SEQS
 NORM_FLOOR = 1e-12
-SCALAR_HEADS = 2
+SHIFTED_BY_VECTOR = ((0, 0), (1, 1), (2, 1))
+SCALAR_HEADS = 1
 SQUARE = 32
 TINY = 1e-30
 
@@ -143,12 +144,14 @@ def tile_full_tmix_params_pa_kernel(tc, x, x_k, W_k, a_hid, a2, a0, k_k, k_a, ou
         def mix_channels(x_t, g, t, planes):
             shifted = shifted_ring[len(mixes) % len(shifted_ring)]
             mixes.append((g, t))
-            nc.scalar.activation(
-                out=shifted[:, :, 1:T],
-                in_=x_t[:].rearrange("p (b r) -> p b r", b=SEQS)[:, :, 0 : T - 1],
-                func=ACT.Copy,
-                scale=mix[:, t, g : g + 1],
-            )
+            previous = x_t[:].rearrange("p (b r) -> p b r", b=SEQS)[:, :, 0 : T - 1]
+            factor = mix[:, t, g : g + 1]
+            if (g, t) in SHIFTED_BY_VECTOR:
+                nc.vector.tensor_scalar(
+                    out=shifted[:, :, 1:T], in0=previous, scalar1=factor, scalar2=None, op0=ALU.mult
+                )
+            else:
+                nc.scalar.activation(out=shifted[:, :, 1:T], in_=previous, func=ACT.Copy, scale=factor)
             nc.vector.scalar_tensor_tensor(
                 out=planes[:, t, :],
                 in0=x_t[:],
@@ -158,12 +161,22 @@ def tile_full_tmix_params_pa_kernel(tc, x, x_k, W_k, a_hid, a2, a0, k_k, k_a, ou
                 op1=ALU.add,
             )
 
-        def regroup_tokens(planes):
+        def regroup_tokens(planes, on_gpsimd):
             grouped = stage.tile([P, TOKENS * PACK], BF16, align_bytes=64)
-            nc.vector.tensor_copy(
-                out=grouped[:].rearrange("p (c i t) -> p c t i", i=4, t=PACK),
-                in_=planes[:].rearrange("p t (c i) -> p c t i", i=4),
-            )
+            if on_gpsimd:
+                nc.gpsimd.tensor_scalar(
+                    out=grouped[:].rearrange("p (c t) -> p c t", t=PACK),
+                    in0=planes[:].rearrange("p t c -> p c t"),
+                    scalar1=1.0,
+                    scalar2=0.0,
+                    op0=ALU.mult,
+                    op1=ALU.add,
+                )
+            else:
+                nc.vector.tensor_copy(
+                    out=grouped[:].rearrange("p (c i t) -> p c t i", i=4, t=PACK),
+                    in_=planes[:].rearrange("p t (c i) -> p c t i", i=4),
+                )
             return grouped
 
         def quantise_tokens(g, grouped):
@@ -347,11 +360,14 @@ def tile_full_tmix_params_pa_kernel(tc, x, x_k, W_k, a_hid, a2, a0, k_k, k_a, ou
             for g in range(PASSES):
                 planes.append(stage.tile([P, PACK, TOKENS], BF16, name="planes"))
                 for i in range(PACK):
+                    if i == PACK - 1:
+                        for w in range([0,0,2,4][g]):
+                            weigh_gate(weighed.pop(0))
                     mix_channels(transpose_tokens(early, g, i), g, i, planes[g])
-                    if i == 0 and g > 0:
-                        grouped.append(regroup_tokens(planes[g - 1]))
-                    if i == 2 and g > 1:
-                        quantise_tokens(g - 2, grouped[g - 2])
+                    if i == PACK - 1 and g > 0:
+                        quantise_tokens(g - 1, grouped[g - 1])
+                    if i == PACK - 1 and g < PASSES - 1:
+                        grouped.append(regroup_tokens(planes[g], True))
                     if g == 0 and i == 0:
                         hid_ps = early.tile([P, TOKENS], BF16, tag="z", bufs=2)
                         for b in range(SEQS):
@@ -359,16 +375,13 @@ def tile_full_tmix_params_pa_kernel(tc, x, x_k, W_k, a_hid, a2, a0, k_k, k_a, ou
                         nc.vector.tensor_copy(out=hid_t[:], in_=hid_ps[:])
                     if g > 0 or i > 2:
                         make_gate(early)
-                    if g > 1 and i > 0:
-                        weigh_gate(weighed.pop(0))
                 if g > 2:
                     w_grouped.append(regroup_weights(early, len(w_grouped), nc.scalar.copy))
             w_grouped.append(regroup_weights(early, len(w_grouped), nc.scalar.copy))
-            quantise_tokens(PASSES - 2, grouped[PASSES - 2])
-            grouped.append(regroup_tokens(planes[PASSES - 1]))
+            quantise_weights()
+            grouped.append(regroup_tokens(planes[PASSES - 1], False))
             quantise_weights()
             quantise_tokens(PASSES - 1, grouped[PASSES - 1])
-            quantise_weights()
             while len(w_grouped) < EARLY_UNITS:
                 w_grouped.append(regroup_weights(early, len(w_grouped), nc.scalar.copy))
                 quantise_weights()

from contextlib import ExitStack

import concourse.mybir as mybir

BF16 = mybir.dt.bfloat16
F32 = mybir.dt.float32
U32 = mybir.dt.uint32
U8 = mybir.dt.uint8
FP8X4 = mybir.dt.float8_e4m3fn_x4
ACT = mybir.ActivationFunctionType
ALU = mybir.AluOpType

P = 128
SEQS = 4
T = 128
TOKENS = SEQS * T
C = 2048
CO = 2048
DA = 128
HEAD = 64
PACK = 4
K_PASS = P * PACK
PASSES = C // K_PASS
WORDS = K_PASS // 2
N_TILE = 512
N_TILES = CO // N_TILE
BLOCKS = N_TILE // P
HEADS = N_TILE // HEAD
BANK_WORDS = 512
BANKS = 8
UNITS = N_TILES * PASSES
EARLY_UNITS = 5
STEPS = N_TILES * SEQS
NORM_FLOOR = 1e-12
SHIFTED_BY_VECTOR = ((0, 0), (1, 1), (2, 1))
SCALAR_HEADS = 1
SQUARE = 32
TINY = 1e-30

FLOPS = 2 * TOKENS * C * CO + 2 * TOKENS * DA * CO


def tile_full_tmix_params_pa_kernel(tc, x, x_k, W_k, a_hid, a2, a0, k_k, k_a, out_0, out_1):
    nc = tc.nc
    with ExitStack() as ctx:
        ctx.enter_context(tc.manual_schedule())
        keep = ctx.enter_context(tc.tile_pool(name="keep", bufs=1))
        x_pool = ctx.enter_context(tc.tile_pool(name="x_pool", bufs=PASSES))
        w_pool = ctx.enter_context(tc.tile_pool(name="w_pool", bufs=10))
        stage = ctx.enter_context(tc.tile_pool(name="stage", bufs=2))
        wq_pool = ctx.enter_context(tc.tile_pool(name="wq_pool", bufs=2 * PASSES + 2))
        gate_pool = ctx.enter_context(tc.tile_pool(name="gate_pool", bufs=STEPS))
        tail = ctx.enter_context(tc.tile_pool(name="tail", bufs=3))

        warm = keep.tile([P, 2], F32)
        nc.vector.memset(warm[:], 1.0)
        nc.scalar.activation(out=warm[:, 1:2], in_=warm[:, 0:1], func=ACT.Sigmoid)

        ones = keep.tile([P, P], F32)
        nc.vector.memset(ones[:], 1.0)

        mix_rows = keep.tile([P, K_PASS], BF16)
        nc.vector.memset(mix_rows[:], 0.0)
        a0_rows = keep.tile([P, P], BF16)
        nc.vector.memset(a0_rows[:], 0.0)

        columns_of = keep.tile([P, P], F32, align_bytes=64)
        nc.vector.tensor_tensor_scan(
            out=columns_of[:], data0=ones[:], data1=ones[:], initial=-1.0, op0=ALU.mult, op1=ALU.add
        )
        rows_of = keep.tile([P, P], F32, align_bytes=64)
        nc.vector.transpose(out=rows_of[:], in_=columns_of[:])
        ident_bf = keep.tile([P, P], BF16)
        for block in range(0, P, SQUARE):
            lines = slice(block, block + SQUARE)
            nc.vector.tensor_scalar(
                out=ident_bf[lines, :],
                in0=columns_of[lines, :],
                scalar1=rows_of[lines, 0:1],
                scalar2=float(block),
                op0=ALU.subtract,
                op1=ALU.is_equal,
            )
        ident_f32 = keep.tile([P, P], F32)
        nc.vector.tensor_copy(out=ident_f32[:], in_=ident_bf[:])
        hid = keep.tile([P, SEQS, DA], BF16)
        a2_sb = keep.tile([DA, CO], BF16)
        k_k_all = keep.tile([P, CO], BF16)
        k_a_all = keep.tile([P, CO], BF16)


        def load_on_all(tile, vector, n):
            columns = slice(n * N_TILE, (n + 1) * N_TILE)
            nc.sync.dma_start(
                out=tile[:, columns], in_=vector.rearrange("a b c -> (a b c)")[columns].partition_broadcast(P)
            )

        x_tiles = []
        for g in range(PASSES):
            x_g = x_pool.tile([P, SEQS, K_PASS], BF16, name="x_g")
            nc.sync.dma_start(out=x_g[:], in_=x[:, :, g * K_PASS : (g + 1) * K_PASS].rearrange("b t c -> t b c"))
            x_tiles.append(x_g)
            if g == 0:
                nc.sync.dma_start(out=mix_rows[0:PASSES, :], in_=x_k.rearrange("a b (r c) -> (a b r) c", c=K_PASS))
                nc.sync.dma_start(out=a0_rows[0 : CO // P, :], in_=a0.rearrange("a b (j p) -> (a b j) p", p=P))
            if g > 1:
                load_on_all(k_a_all, k_a, g - 2)
            if g == 0:
                nc.sync.dma_start(out=hid[:], in_=a_hid.rearrange("b t d -> t b d"))
                nc.sync.dma_start(out=a2_sb[:], in_=a2)
        w_tiles = []
        for i in range(CO // P):
            w_i = w_pool.tile([P, C], BF16, name="w_i")
            nc.sync.dma_start(out=w_i[:], in_=W_k[i * P : (i + 1) * P, :])
            w_tiles.append(w_i)
            if i % BLOCKS == BLOCKS - 1:
                load_on_all(k_k_all, k_k, i // BLOCKS)
                if i // BLOCKS + 2 < N_TILES:
                    load_on_all(k_a_all, k_a, i // BLOCKS + 2)

        mix = keep.tile([P, PACK, PASSES], F32)
        stay = keep.tile([P, PACK, PASSES], F32)
        hid_t = keep.tile([DA, TOKENS], BF16)
        xk_codes = keep.tile([P, PASSES, TOKENS], U32, align_bytes=64)
        xk_scales = keep.tile([P, PASSES, TOKENS], U8, align_bytes=64)
        shifted_ring = [keep.tile([P, SEQS, T], F32, name="shifted%d" % i) for i in range(3)]
        for shifted in shifted_ring:
            nc.vector.memset(shifted[:, :, 0:1], 0.0)

        def transpose_tokens(banks, g, t):
            x_t = banks.tile([P, TOKENS], BF16, tag="x", bufs=3)
            for b in range(SEQS):
                nc.tensor.transpose(x_t[:, b * T : (b + 1) * T], x_tiles[g][:, b, t:K_PASS:PACK], ident_bf[:])
            return x_t

        zeros = keep.tile([P, HEADS, 2], F32)
        nc.vector.memset(zeros[:], 0.0)
        inverse_ring = [keep.tile([P, HEADS, 2], F32, name="inverses%d" % i) for i in range(4)]
        for inverses in inverse_ring:
            nc.vector.tensor_scalar_add(out=inverses[:], in0=zeros[:], scalar1=1.0 / NORM_FLOOR)
        tiny = keep.tile([P, 1], F32)
        nc.vector.tensor_scalar_add(out=tiny[:], in0=zeros[:, 0, 0:1], scalar1=TINY)

        def mix_channels(x_t, g, t, planes):
            shifted = shifted_ring[len(mixes) % len(shifted_ring)]
            mixes.append((g, t))
            previous = x_t[:].rearrange("p (b r) -> p b r", b=SEQS)[:, :, 0 : T - 1]
            factor = mix[:, t, g : g + 1]
            if (g, t) in SHIFTED_BY_VECTOR:
                nc.vector.tensor_scalar(
                    out=shifted[:, :, 1:T], in0=previous, scalar1=factor, scalar2=None, op0=ALU.mult
                )
            else:
                nc.scalar.activation(out=shifted[:, :, 1:T], in_=previous, func=ACT.Copy, scale=factor)
            nc.vector.scalar_tensor_tensor(
                out=planes[:, t, :],
                in0=x_t[:],
                scalar=stay[:, t, g : g + 1],
                in1=shifted[:].rearrange("p b r -> p (b r)"),
                op0=ALU.mult,
                op1=ALU.add,
            )

        def regroup_tokens(planes, on_gpsimd):
            grouped = stage.tile([P, TOKENS * PACK], BF16, align_bytes=64)
            if on_gpsimd:
                nc.gpsimd.tensor_scalar(
                    out=grouped[:].rearrange("p (c t) -> p c t", t=PACK),
                    in0=planes[:].rearrange("p t c -> p c t"),
                    scalar1=1.0,
                    scalar2=0.0,
                    op0=ALU.mult,
                    op1=ALU.add,
                )
            else:
                nc.vector.tensor_copy(
                    out=grouped[:].rearrange("p (c i t) -> p c t i", i=4, t=PACK),
                    in_=planes[:].rearrange("p t (c i) -> p c t i", i=4),
                )
            return grouped

        def quantise_tokens(g, grouped):
            nc.vector.quantize_mx(out=xk_codes[:, g, :].bitcast(FP8X4), scales=xk_scales[:, g, :], in_=grouped[:])

        def regroup_weights(banks, unit, copy):
            n, g = divmod(unit, PASSES)
            w_grouped = stage.tile([P, N_TILE * PACK], BF16, align_bytes=64, bufs=4)
            words = w_grouped[:].bitcast(F32)
            for h in range(BLOCKS // 2):
                w_t = banks.tile([P, 2, 2 * P], F32, tag="w")
                for u in range(2):
                    for i in range(2):
                        nc.tensor.transpose(
                            w_t[:, u, i * P : (i + 1) * P],
                            w_tiles[n * BLOCKS + 2 * h + i][:].bitcast(F32)[:, g * WORDS + u : (g + 1) * WORDS : 2],
                            ident_f32[:],
                        )
                copy(
                    out=words[:, h * BANK_WORDS : (h + 1) * BANK_WORDS].rearrange("p (c u) -> p c u", u=2),
                    in_=w_t[:].rearrange("p u c -> p c u"),
                )
            return w_grouped

        def quantise_weights():
            w_codes = wq_pool.tile([P, N_TILE], U32, align_bytes=64)
            w_scales = wq_pool.tile([P, N_TILE], U8, align_bytes=64)
            nc.vector.quantize_mx(out=w_codes[:].bitcast(FP8X4), scales=w_scales[:], in_=w_grouped[len(quantised)][:])
            quantised.append((w_codes, w_scales))

        def make_gate(banks, z_bufs=2):
            n, b = divmod(len(gates), SEQS)
            z_ps = banks.tile([P, N_TILE], F32, tag="z", bufs=z_bufs)
            nc.tensor.matmul(
                z_ps[:],
                lhsT=hid_t[:, b * T : (b + 1) * T],
                rhs=a2_sb[:, n * N_TILE : (n + 1) * N_TILE],
                start=True,
                stop=False,
            )
            for i in range(BLOCKS):
                j = n * BLOCKS + i
                nc.tensor.matmul(
                    z_ps[:, i * P : (i + 1) * P],
                    lhsT=a0_one[:, j : j + 1].to_broadcast([P, P]),
                    rhs=ident_f32[:],
                    is_transpose=True,
                    start=False,
                    stop=(i == BLOCKS - 1),
                )
            gate = gate_pool.tile([P, N_TILE], F32)
            nc.scalar.activation(out=gate[:], in_=z_ps[:], func=ACT.Sigmoid, scale=-1.0)
            gates.append(gate)

        def weigh_gate(step):
            n = step // SEQS
            nc.vector.scalar_tensor_tensor(
                out=gates[step][:],
                in0=gates[step][:],
                scalar=-1.0,
                in1=k_a_all[:, n * N_TILE : (n + 1) * N_TILE],
                op0=ALU.mult,
                op1=ALU.mult,
            )

        def multiply(sums, n, b):
            k_ps = sums.tile([P, N_TILE], F32)
            for g in range(PASSES):
                w_codes, w_scales = quantised[n * PASSES + g]
                nc.tensor.matmul_mx(
                    out=k_ps[:],
                    lhsT=xk_codes[:, g, b * T : (b + 1) * T].bitcast(FP8X4),
                    lhsT_scale=xk_scales[:, g, b * T : (b + 1) * T],
                    rhs=w_codes[:].bitcast(FP8X4),
                    rhs_scale=w_scales[:],
                    start=(g == 0),
                    stop=(g == PASSES - 1),
                )
            return k_ps

        def scale_by_k_k(n, k_ps):
            scaled = tail.tile([P, N_TILE], F32, bufs=6)
            nc.vector.tensor_tensor(
                out=scaled[:], in0=k_ps[:], in1=k_k_all[:, n * N_TILE : (n + 1) * N_TILE], op=ALU.mult
            )
            return scaled

        def sum_squares_on_scalar(step, scaled, heads):
            sums_of = tail.tile([P, HEADS], F32, name="sums_of", bufs=3)
            squares = tail.tile([P, N_TILE], F32, bufs=3)
            for h in range(heads):
                nc.scalar.activation(
                    out=squares[:, h * HEAD : (h + 1) * HEAD],
                    in_=scaled[:, h * HEAD : (h + 1) * HEAD],
                    func=ACT.Square,
                    accum_out=sums_of[:, h : h + 1],
                )
            return sums_of

        def square(scaled, head):
            squares = tail.tile([P, N_TILE], F32, bufs=3)
            columns = slice(head * HEAD, N_TILE)
            nc.scalar.activation(out=squares[:, columns], in_=scaled[:, columns], func=ACT.Square)
            return squares

        def sum_squares_on_vector(sums_of, squares, head):
            nc.vector.tensor_reduce(
                out=sums_of[:, head:HEADS],
                in_=squares[:, head * HEAD : N_TILE].rearrange("p (h d) -> p h d", d=HEAD),
                axis=mybir.AxisListType.X,
                op=ALU.add,
            )

        def store_k_out(n, b, k_ps, gate):
            k_out = tail.tile([P, N_TILE], F32, bufs=5)
            nc.vector.scalar_tensor_tensor(
                out=k_out[:], in0=gate[:], scalar=1.0, in1=k_ps[:], op0=ALU.add, op1=ALU.mult
            )
            nc.sync.dma_start(out=out_0[b, :, n * N_TILE : (n + 1) * N_TILE], in_=k_out[:])

        def invert_norm(step, sums_of):
            inverses = inverse_ring[step % len(inverse_ring)]
            nc.scalar.activation(
                out=inverses[:, :, 0], in_=sums_of[:], func=ACT.Abs_reciprocal_sqrt, bias=tiny[:]
            )
            return inverses

        def cap(inverses):
            inv_norm = tail.tile([P, HEADS], F32)
            nc.vector.tensor_reduce(out=inv_norm[:], in_=inverses[:], axis=mybir.AxisListType.X, op=ALU.min)
            return inv_norm

        def store_kk(n, b, scaled, inv_norm):
            kk = tail.tile([P, N_TILE], F32, bufs=5)
            shared = HEADS - SCALAR_HEADS
            columns = slice(0, shared * HEAD)
            nc.gpsimd.tensor_tensor(
                out=kk[:, columns].rearrange("p (h d) -> p h d", d=HEAD),
                in0=scaled[:, columns].rearrange("p (h d) -> p h d", d=HEAD),
                in1=inv_norm[:, 0:shared].unsqueeze(2).to_broadcast([P, shared, HEAD]),
                op=ALU.mult,
            )
            for h in range(shared, HEADS):
                columns = slice(h * HEAD, (h + 1) * HEAD)
                nc.scalar.activation(
                    out=kk[:, columns], in_=scaled[:, columns], func=ACT.Copy, scale=inv_norm[:, h : h + 1]
                )
            nc.sync.dma_start(out=out_1[b, :, n * N_TILE : (n + 1) * N_TILE], in_=kk[:])

        def cap_and_store_kk(n, b, scaled, inverses):
            kk = tail.tile([P, N_TILE], F32, bufs=5)
            nc.vector.scalar_tensor_tensor(
                out=kk[:].rearrange("p (h d) -> p h d", d=HEAD),
                in0=inverses[:, :, 0:1].to_broadcast([P, HEADS, HEAD]),
                scalar=1.0 / NORM_FLOOR,
                in1=scaled[:].rearrange("p (h d) -> p h d", d=HEAD),
                op0=ALU.min,
                op1=ALU.mult,
            )
            nc.sync.dma_start(out=out_1[b, :, n * N_TILE : (n + 1) * N_TILE], in_=kk[:])

        w_grouped = []
        quantised = []
        gates = []
        mixes = []

        with tc.psum_pool(name="early", bufs=3) as early:
            mix_ps = early.tile([P, PACK, P], BF16, tag="x", bufs=3)
            for t in range(PACK):
                nc.tensor.transpose(mix_ps[:, t, :], mix_rows[:, t:K_PASS:PACK], ident_bf[:])
            nc.vector.tensor_copy(out=mix[:], in_=mix_ps[:, :, 0:PASSES])
            nc.vector.tensor_scalar(
                out=stay[:], in0=mix_ps[:, :, 0:PASSES], scalar1=-1.0, scalar2=1.0, op0=ALU.mult, op1=ALU.add
            )
            a0_ps = early.tile([P, P], BF16, tag="z", bufs=2)
            nc.tensor.transpose(a0_ps[:], a0_rows[:], ident_bf[:])
            a0_one = keep.tile([P, CO // P], F32)
            nc.vector.tensor_copy(out=a0_one[:], in_=a0_ps[:, 0 : CO // P])
            planes, grouped = [], []
            weighed = list(range(STEPS))
            for g in range(PASSES):
                planes.append(stage.tile([P, PACK, TOKENS], BF16, name="planes"))
                for i in range(PACK):
                    if i == PACK - 1:
                        for w in range([0,0,2,4][g]):
                            weigh_gate(weighed.pop(0))
                    mix_channels(transpose_tokens(early, g, i), g, i, planes[g])
                    if i == PACK - 1 and g > 0:
                        quantise_tokens(g - 1, grouped[g - 1])
                    if i == PACK - 1 and g < PASSES - 1:
                        grouped.append(regroup_tokens(planes[g], True))
                    if g == 0 and i == 0:
                        hid_ps = early.tile([P, TOKENS], BF16, tag="z", bufs=2)
                        for b in range(SEQS):
                            nc.tensor.transpose(hid_ps[:, b * T : (b + 1) * T], hid[:, b, :], ident_bf[:])
                        nc.vector.tensor_copy(out=hid_t[:], in_=hid_ps[:])
                    if g > 0 or i > 2:
                        make_gate(early)
                if g > 2:
                    w_grouped.append(regroup_weights(early, len(w_grouped), nc.scalar.copy))
            w_grouped.append(regroup_weights(early, len(w_grouped), nc.scalar.copy))
            quantise_weights()
            grouped.append(regroup_tokens(planes[PASSES - 1], False))
            quantise_weights()
            quantise_tokens(PASSES - 1, grouped[PASSES - 1])
            while len(w_grouped) < EARLY_UNITS:
                w_grouped.append(regroup_weights(early, len(w_grouped), nc.scalar.copy))
                quantise_weights()
                if len(gates) < STEPS:
                    make_gate(early)
            while len(quantised) < EARLY_UNITS:
                quantise_weights()
            nc.scalar.activation(out=warm[:, 1:2], in_=warm[:, 0:1], func=ACT.Abs_reciprocal_sqrt)

        with tc.psum_pool(name="work", bufs=3, reuse_waits="tile") as work, tc.psum_pool(
            name="sums", bufs=4, reuse_waits="tile"
        ) as sums:
            summed = None
            for step in range(STEPS):
                n, b = divmod(step, SEQS)
                last = step == STEPS - 1
                k_ps = multiply(sums, n, b)
                if len(w_grouped) < UNITS:
                    w_grouped.append(regroup_weights(work, len(w_grouped), nc.scalar.copy))
                if summed is not None:
                    inverses = invert_norm(step - 1, summed[3])
                scaled = scale_by_k_k(n, k_ps)
                half = HEADS // 2 if last else HEADS
                if last:
                    squares = square(scaled, half)
                sums_of = sum_squares_on_scalar(step, scaled, half)
                store_k_out(n, b, k_ps, gates[step])
                if summed is not None and not last:
                    store_kk(*summed[0:3], cap(inverses))
                if not last:
                    if weighed:
                        weigh_gate(weighed.pop(0))
                if len(quantised) < UNITS:
                    quantise_weights()
                before = summed
                summed = (n, b, scaled, sums_of)
            sum_squares_on_vector(sums_of, squares, half)
            last_inverses = invert_norm(step, sums_of)
            cap_and_store_kk(*before[0:3], inverses)
            cap_and_store_kk(n, b, scaled, last_inverses)
